import numpy as np
import ml_dtypes


def mxq(x, axis, fmt="e4m3"):
    dtype, down = {"e4m3": (ml_dtypes.float8_e4m3fn, 7), "e5m2": (ml_dtypes.float8_e5m2, 14)}[fmt]
    v = np.moveaxis(np.asarray(x, np.float32).astype(ml_dtypes.bfloat16).astype(np.float64), axis, -1)
    blocks = v.reshape(v.shape[:-1] + (-1, 32))
    amax = np.abs(blocks).max(-1, keepdims=True)
    byte = np.maximum(np.where(amax > 0, np.frexp(amax)[1] - 1 + 127, 0) - down, 1)
    scale = np.exp2(byte - 127.0)
    codes = (blocks / scale).astype(np.float32).astype(dtype).astype(np.float64)
    return np.moveaxis((codes * scale).reshape(v.shape), -1, axis)


WIDE = False


def mx_kscale(k):
    if not WIDE:
        return np.ones(k)
    levels = np.array([10, -10, 5, -5, 0])
    if k % 512:
        return np.exp2(np.random.permutation(np.resize(levels, k // 32))).repeat(32)
    a = np.empty((k // 512, 16))
    for p in range(k // 512):
        a[p, :8] = np.random.permutation(np.resize(levels, 8))
        for g in range(8):
            far = levels[np.abs(levels - a[p, g]) >= 10]
            a[p, g + 8] = far[np.random.randint(len(far))]
    return np.exp2(a.ravel()).repeat(32)


BF16 = ml_dtypes.bfloat16


def bf(x):
    return np.asarray(x, np.float32).astype(BF16)


def f64(x):
    return np.asarray(x).astype(np.float64)


S, A, B, K, H, G = 4, 8, 16, 1024, 1024, 3


def sigmoid(v):
    return 1.0 / (1.0 + np.exp(-v))


def draw0():
    s = mx_kscale(K)
    c = 0.7 / np.sqrt(K)
    return {"x": bf(np.random.standard_normal((S + 1, A, B, K)) * s),
            "x_mix": bf(np.random.standard_normal((S + 1, A, B, H))),
            "WL": bf(np.random.standard_normal((H, K)) * c / s),
            "WR": bf(np.random.standard_normal((H, K)) * c / s),
            "GL": bf(np.random.standard_normal((G * H, K)) * c / s),
            "GR": bf(np.random.standard_normal((G * H, K)) * c / s)}


def core(x, x_mix, WL, WR, GL, GR):
    xm = f64(x_mix)
    left, right = xm[:-1], xm[1:]
    xq = mxq(f64(x), 3, "e4m3")
    lq, rq = xq[:-1], xq[1:]
    center = sigmoid((lq @ mxq(f64(WL), 1, "e4m3").T) + (rq @ mxq(f64(WR), 1, "e4m3").T))
    gate = (lq @ mxq(f64(GL), 1, "e4m3").T) + (rq @ mxq(f64(GR), 1, "e4m3").T)
    g = gate.reshape(gate.shape[:-1] + (G, H))
    e = np.exp(g - g.max(-2, keepdims=True))
    w = e / e.sum(-2, keepdims=True)
    return left * w[..., 0, :] + right * w[..., 1, :] + center * w[..., 2, :]


def e4m3fn_bytes(y):
    return np.clip(np.asarray(y, np.float64), -448.0, 448.0).astype(np.float32).astype(ml_dtypes.float8_e4m3fn).view(np.uint8)


def e4m3fn_values(b):
    return np.asarray(b, np.uint8).view(ml_dtypes.float8_e4m3fn).astype(np.float64)


def setup_inputs():
    d = draw0()
    x0 = np.asarray(d['GR']).astype(np.float64)
    s = (np.max(np.abs(x0), axis=(0,), keepdims=True) / 448.0).astype(np.float32)
    out = {}
    for k, v in d.items():
        if k == 'GR':
            out['GR_bytes'] = e4m3fn_bytes(x0 / s.astype(np.float64))
            out['GR_scale'] = s
        else:
            out[k] = v
    return out


def reference(x, x_mix, WL, WR, GL, GR_bytes, GR_scale):
    return core(x, x_mix, WL, WR, GL, e4m3fn_values(GR_bytes) * GR_scale.astype(np.float64))

@@ -1,0 +1,286 @@
+from contextlib import ExitStack
+
+import concourse.mybir as mybir
+from concourse.masks import make_identity
+
+FLOPS = 2 * 512 * 4096 * 2048
+
+F32 = mybir.dt.float32
+BF16 = mybir.dt.bfloat16
+U32 = mybir.dt.uint32
+U8 = mybir.dt.uint8
+FP8 = mybir.dt.float8_e4m3fn
+FP8X4 = mybir.dt.float8_e4m3fn_x4
+ALU = mybir.AluOpType
+ACT = mybir.ActivationFunctionType
+
+P = 128
+K = 1024
+HALF = 512
+TILES = 4
+POSITIONS = 4
+
+PAIR_ORDER = (("g1", 0), ("zc", 0), ("g0", 0), ("g1", 1), ("g0", 1), ("g2", 0), ("zc", 1), ("g2", 1))
+
+
+def tile_grconv_pa_kernel(tc, x, x_mix, WL, WR, GL, GR_bytes, GR_scale, out):
+    nc = tc.nc
+    with ExitStack() as ctx:
+        const = ctx.enter_context(tc.tile_pool(name="const", bufs=1))
+        rows_pool = ctx.enter_context(tc.tile_pool(name="rows_pool", bufs=4))
+        bytes_pool = ctx.enter_context(tc.tile_pool(name="bytes_pool", bufs=4))
+        wide_pool = ctx.enter_context(tc.tile_pool(name="wide_pool", bufs=3))
+        grouped_pool = ctx.enter_context(tc.tile_pool(name="grouped_pool", bufs=3))
+        codes_pool = ctx.enter_context(tc.tile_pool(name="codes_pool", bufs=6))
+        mix_pool = ctx.enter_context(tc.tile_pool(name="mix_pool", bufs=2))
+        turn_psum = ctx.enter_context(tc.psum_pool(name="turn_psum", bufs=4))
+        plane_psum = ctx.enter_context(tc.psum_pool(name="plane_psum", bufs=4))
+
+        x_view = x.rearrange("s a b k -> (a b) s k")
+        mix_view = x_mix.rearrange("s a b h -> (a b) s h")
+        out_view = out.rearrange("s a b h -> (a b) s h")
+
+        ident_f32 = const.tile([P, P], F32, name="ident_f32")
+        make_identity(nc, ident_f32[:])
+        ident_bf16 = const.tile([P, P], BF16, name="ident_bf16")
+        make_identity(nc, ident_bf16[:])
+        minus_ident = const.tile([P, P], BF16, name="minus_ident")
+        nc.vector.tensor_scalar(out=minus_ident[:], in0=ident_bf16[:], scalar1=-1.0, scalar2=None, op0=ALU.mult)
+        zero_col = const.tile([P, 1], F32, name="zero_col")
+        nc.gpsimd.memset(zero_col[:], 0.0)
+        table_warm = const.tile([P, 1], F32, name="table_warm")
+        nc.scalar.activation(out=table_warm[:], in_=zero_col[:], func=ACT.Sigmoid)
+
+        scales = const.tile([P, 2, K], F32, name="scales")
+        nc.sync.dma_start(out=scales[:, 0, :], in_=GR_scale.rearrange("o k -> (o k)").partition_broadcast(P))
+        nc.scalar.copy(out=scales[:, 1, :], in_=scales[:, 0, :])
+        mix_rows = const.tile([P, POSITIONS + 1, K], BF16, name="mix_rows")
+
+        def weight_group(name, dram, first_row, from_bytes):
+            return {
+                "name": name,
+                "src": dram[first_row : first_row + HALF, :].rearrange("(i p) k -> p i k", p=P),
+                "from_bytes": from_bytes,
+                "tiles": TILES,
+            }
+
+        x_first = {"name": "x_first", "src": x_view[:, 0:4, :], "from_bytes": False, "tiles": 4}
+        x_last = {"name": "x_last", "src": x_view[:, 4:5, :], "from_bytes": False, "tiles": 1}
+
+        def make_pair(kind, half):
+            if kind == "zc":
+                first_row = half * HALF
+                return (
+                    kind,
+                    half,
+                    weight_group("wl_%d" % half, WL, first_row, False),
+                    weight_group("wr_%d" % half, WR, first_row, False),
+                )
+            first_row = int(kind[1]) * 1024 + half * HALF
+            return (
+                kind,
+                half,
+                weight_group("gl_%s_%d" % (kind, half), GL, first_row, False),
+                weight_group("gr_%s_%d" % (kind, half), GR_bytes, first_row, True),
+            )
+
+        pairs = [make_pair(kind, half) for kind, half in PAIR_ORDER]
+        weight_groups = []
+        for pr in pairs:
+            weight_groups.extend([pr[2], pr[3]])
+        rows_to_load = [x_first, x_last] + [g for g in weight_groups if not g["from_bytes"]]
+        bytes_to_load = [g for g in weight_groups if g["from_bytes"]]
+        piecewise = (x_first["name"], pairs[0][2]["name"], pairs[0][3]["name"])
+        mix_follows = pairs[2][2]["name"]
+
+        def load(dst, g):
+            if g["name"] in piecewise:
+                for i in range(g["tiles"]):
+                    nc.sync.dma_start(out=dst[:, i, :], in_=g["src"][:, i, :])
+            else:
+                nc.sync.dma_start(out=dst[:], in_=g["src"])
+
+        def load_next_rows():
+            if not rows_to_load:
+                return
+            g = rows_to_load.pop(0)
+            rows = rows_pool.tile([P, g["tiles"], K], BF16, name="rows", tag="rows")
+            load(rows, g)
+            g["rows"] = rows
+            if g["name"] == mix_follows:
+                nc.sync.dma_start(out=mix_rows[:], in_=mix_view)
+
+        def load_next_bytes():
+            if not bytes_to_load:
+                return
+            g = bytes_to_load.pop(0)
+            gr_bytes = bytes_pool.tile([P, TILES, K], U8, name="gr_bytes", tag="gr_bytes")
+            load(gr_bytes, g)
+            g["gr_bytes"] = gr_bytes
+
+        def widen(g):
+            wide = wide_pool.tile([P, TILES, K], BF16, name="wide", tag="wide")
+            step = 1 if g["name"] in piecewise else 2
+            for i in range(0, TILES, step):
+                nc.vector.tensor_tensor(
+                    out=wide[:, i : i + step, :],
+                    in0=g["gr_bytes"][:, i : i + step, :].bitcast(FP8),
+                    in1=scales[:, 0:step, :],
+                    op=ALU.mult,
+                )
+            g["rows"] = wide
+            load_next_bytes()
+
+        def turn(g):
+            n = g["tiles"]
+            grouped = grouped_pool.tile([P, n * K], BF16, name="grouped", tag="grouped", align_bytes=64)
+            grouped_words = grouped[:].bitcast(F32).rearrange("p (g i r u) -> p g i r u", g=2, i=n, u=2)
+            for i in range(n):
+                words = g["rows"][:, i, :].bitcast(F32)
+                bank = turn_psum.tile([P, 512], F32, name="bank", tag="bank")
+                for g2 in range(2):
+                    for u in range(2):
+                        c = 2 * g2 + u
+                        nc.tensor.transpose(
+                            bank[:, c * P : (c + 1) * P],
+                            words[:, 256 * g2 + u : 256 * (g2 + 1) : 2],
+                            ident_f32[:],
+                        )
+                nc.scalar.copy(
+                    out=grouped_words[:, :, i, :, :],
+                    in_=bank[:].rearrange("p (g u r) -> p g r u", g=2, u=2),
+                )
+            if not g["from_bytes"]:
+                load_next_rows()
+            g["grouped"] = grouped
+
+        def quantise(g, pool):
+            n = g["tiles"]
+            if pool is const:
+                codes = pool.tile([P, n * 256], U32, name="codes_" + g["name"], align_bytes=64)
+                blocks = pool.tile([P, n * 256], U8, name="blocks_" + g["name"], align_bytes=64)
+            else:
+                codes = pool.tile([P, n * 256], U32, name="codes", tag="codes", align_bytes=64)
+                blocks = pool.tile([P, n * 256], U8, name="blocks", tag="blocks", align_bytes=64)
+            nc.vector.quantize_mx(out=codes[:].bitcast(FP8X4), scales=blocks[:], in_=g["grouped"][:])
+            g["codes"] = codes
+            g["blocks"] = blocks
+
+        def prepare(g, pool):
+            if g["from_bytes"]:
+                widen(g)
+            turn(g)
+            quantise(g, pool)
+
+        def x_operand(pos, g2):
+            if pos < 4:
+                lo = g2 * 512 + pos * P
+                return x_first["codes"][:, lo : lo + P], x_first["blocks"][:, lo : lo + P]
+            lo = g2 * P
+            return x_last["codes"][:, lo : lo + P], x_last["blocks"][:, lo : lo + P]
+
+        def plane(s, left_group, right_group):
+            acc = plane_psum.tile([P, HALF], F32, name="acc", tag="acc")
+            passes = [(s, 0, left_group), (s, 1, left_group), (s + 1, 0, right_group), (s + 1, 1, right_group)]
+            for n, (pos, g2, grp) in enumerate(passes):
+                x_codes, x_blocks = x_operand(pos, g2)
+                nc.tensor.matmul_mx(
+                    out=acc[:],
+                    lhsT=x_codes.bitcast(FP8X4),
+                    lhsT_scale=x_blocks,
+                    rhs=grp["codes"][:, g2 * HALF : (g2 + 1) * HALF].bitcast(FP8X4),
+                    rhs_scale=grp["blocks"][:, g2 * HALF : (g2 + 1) * HALF],
+                    start=(n == 0),
+                    stop=(n == 3),
+                )
+            return acc
+
+        mix = {}
+
+        def mix_tile(name, half):
+            t = mix_pool.tile([P, POSITIONS, HALF], F32, name=name, tag=name)
+            mix[(name, half)] = t
+
+        def consume(pr, positions):
+            kind, half, left_group, right_group = pr
+            if positions[0] == 0:
+                if kind == "zc":
+                    mix_tile("c", half)
+                elif kind == "g1":
+                    mix_tile("g1", half)
+                elif kind == "g0":
+                    mix_tile("u", half)
+                    mix_tile("d", half)
+                    mix_tile("m", half)
+            for s in positions:
+                acc = plane(s, left_group, right_group)
+                if kind == "zc":
+                    nc.scalar.activation(out=mix[("c", half)][:, s, :], in_=acc[:], func=ACT.Sigmoid)
+                elif kind == "g1":
+                    nc.scalar.copy(out=mix[("g1", half)][:, s, :], in_=acc[:])
+                elif kind == "g0":
+                    g1, d, m, u = mix[("g1", half)], mix[("d", half)], mix[("m", half)], mix[("u", half)]
+                    nc.vector.tensor_tensor(out=d[:, s, :], in0=acc[:], in1=g1[:, s, :], op=ALU.subtract)
+                    nc.vector.tensor_tensor(out=m[:, s, :], in0=acc[:], in1=g1[:, s, :], op=ALU.max)
+                    nc.scalar.activation(out=d[:, s, :], in_=d[:, s, :], func=ACT.Sigmoid)
+                    nc.scalar.activation(out=u[:, s, :], in_=d[:, s, :], func=ACT.Abs, bias=-0.5)
+                else:
+                    m = mix[("m", half)]
+                    nc.vector.tensor_tensor(out=m[:, s, :], in0=acc[:], in1=m[:, s, :], op=ALU.subtract)
+                    nc.scalar.activation(out=m[:, s, :], in_=m[:, s, :], func=ACT.Sigmoid)
+
+        def in_place(name, half, op, other, sl):
+            t = mix[(name, half)]
+            nc.vector.tensor_tensor(out=t[:, sl, :], in0=t[:, sl, :], in1=other, op=op)
+
+        EVERY = slice(0, POSITIONS)
+
+        def after_g0(half):
+            cols = slice(half * HALF, (half + 1) * HALF)
+            u, d = mix[("u", half)], mix[("d", half)]
+            nc.scalar.activation(out=u[:], in_=u[:], func=ACT.Ln, bias=0.5)
+            for s in range(POSITIONS):
+                diff = plane_psum.tile([P, HALF], F32, name="acc", tag="acc")
+                nc.tensor.matmul(diff[:], lhsT=ident_bf16[:], rhs=mix_rows[:, s, cols], start=True, stop=False)
+                nc.tensor.matmul(diff[:], lhsT=minus_ident[:], rhs=mix_rows[:, s + 1, cols], start=False, stop=True)
+                nc.vector.tensor_tensor(out=d[:, s, :], in0=d[:, s, :], in1=diff[:], op=ALU.mult)
+            in_place("m", half, ALU.subtract, u[:], EVERY)
+            in_place("d", half, ALU.add, mix_rows[:, 1 : POSITIONS + 1, cols], EVERY)
+
+        def finish(half, sl):
+            in_place("c", half, ALU.mult, mix[("m", half)][:, sl, :], sl)
+            in_place("c", half, ALU.add, mix[("d", half)][:, sl, :], sl)
+            nc.sync.dma_start(out=out_view[:, sl, half * HALF : (half + 1) * HALF], in_=mix[("c", half)][:, sl, :])
+
+        load_next_bytes()
+        for n in range(4):
+            load_next_rows()
+        for n in range(3):
+            load_next_bytes()
+
+        prepare(x_first, const)
+        prepare(x_last, const)
+        prepare(weight_groups[0], codes_pool)
+        prepare(weight_groups[1], codes_pool)
+
+        steps = 2 * len(pairs)
+        seen = set()
+        for k in range(steps):
+            pr = pairs[k // 2]
+            kind, half = pr[0], pr[1]
+            first = 2 * (k % 2)
+            if k + 2 < steps:
+                prepare(weight_groups[k + 2], codes_pool)
+            consume(pr, (first, first + 1))
+            if k // 2 == len(pairs) - 1:
+                finish(half, slice(first, first + 2))
+                continue
+            if first == 0:
+                continue
+            seen.add((kind, half))
+            if kind == "g0":
+                after_g0(half)
+            if kind in ("g0", "zc") and ("g0", half) in seen and ("zc", half) in seen:
+                in_place("c", half, ALU.subtract, mix[("d", half)][:], EVERY)
+            if kind in ("g2", "zc") and ("g2", half) in seen and ("zc", half) in seen:
+                finish(half, EVERY)

@@ -179,8 +179,8 @@ def tile_grconv_pa_kernel(tc, x, x_mix, WL, WR, GL, GR_bytes, GR_scale, out):
             lo = g2 * P
             return x_last["codes"][:, lo : lo + P], x_last["blocks"][:, lo : lo + P]
 
-        def plane(s, left_group, right_group):
-            acc = plane_psum.tile([P, HALF], F32, name="acc", tag="acc")
+        def plane(s, left_group, right_group, lo=0, width=HALF):
+            acc = plane_psum.tile([P, width], F32, name="acc", tag="acc")
             passes = [(s, 0, left_group), (s, 1, left_group), (s + 1, 0, right_group), (s + 1, 1, right_group)]
             for n, (pos, g2, grp) in enumerate(passes):
                 x_codes, x_blocks = x_operand(pos, g2)
@@ -188,8 +188,8 @@ def tile_grconv_pa_kernel(tc, x, x_mix, WL, WR, GL, GR_bytes, GR_scale, out):
                     out=acc[:],
                     lhsT=x_codes.bitcast(FP8X4),
                     lhsT_scale=x_blocks,
-                    rhs=grp["codes"][:, g2 * HALF : (g2 + 1) * HALF].bitcast(FP8X4),
-                    rhs_scale=grp["blocks"][:, g2 * HALF : (g2 + 1) * HALF],
+                    rhs=grp["codes"][:, g2 * HALF + lo : g2 * HALF + lo + width].bitcast(FP8X4),
+                    rhs_scale=grp["blocks"][:, g2 * HALF + lo : g2 * HALF + lo + width],
                     start=(n == 0),
                     stop=(n == 3),
                 )
@@ -247,15 +247,27 @@ def tile_grconv_pa_kernel(tc, x, x_mix, WL, WR, GL, GR_bytes, GR_scale, out):
             in_place("m", half, ALU.subtract, u[:], EVERY)
             in_place("d", half, ALU.add, mix_rows[:, 1 : POSITIONS + 1, cols], EVERY)
 
-        def finish(half, sl):
-            in_place("c", half, ALU.mult, mix[("m", half)][:, sl, :], sl)
-            in_place("c", half, ALU.add, mix[("d", half)][:, sl, :], sl)
-            nc.sync.dma_start(out=out_view[:, sl, half * HALF : (half + 1) * HALF], in_=mix[("c", half)][:, sl, :])
+        def finish(half, sl, lo=0, width=HALF):
+            c, m, d = mix[("c", half)], mix[("m", half)], mix[("d", half)]
+            cols = slice(lo, lo + width)
+            nc.vector.tensor_tensor(out=c[:, sl, cols], in0=c[:, sl, cols], in1=m[:, sl, cols], op=ALU.mult)
+            nc.vector.tensor_tensor(out=c[:, sl, cols], in0=c[:, sl, cols], in1=d[:, sl, cols], op=ALU.add)
+            nc.sync.dma_start(out=out_view[:, sl, half * HALF + lo : half * HALF + lo + width], in_=c[:, sl, cols])
 
+        def last_weight(pr, s, lo, width):
+            kind, half, left_group, right_group = pr
+            acc = plane(s, left_group, right_group, lo, width)
+            m = mix[("m", half)]
+            cols = slice(lo, lo + width)
+            nc.vector.tensor_tensor(out=m[:, s, cols], in0=acc[:], in1=m[:, s, cols], op=ALU.subtract)
+            nc.scalar.activation(out=m[:, s, cols], in_=m[:, s, cols], func=ACT.Sigmoid)
+            finish(half, slice(s, s + 1), lo, width)
+
+        load_next_bytes()
         load_next_bytes()
         for n in range(4):
             load_next_rows()
-        for n in range(3):
+        for n in range(2):
             load_next_bytes()
 
         prepare(x_first, const)
@@ -271,6 +283,11 @@ def tile_grconv_pa_kernel(tc, x, x_mix, WL, WR, GL, GR_bytes, GR_scale, out):
             first = 2 * (k % 2)
             if k + 2 < steps:
                 prepare(weight_groups[k + 2], codes_pool)
+            if k == steps - 1:
+                last_weight(pr, first, 0, HALF)
+                last_weight(pr, first + 1, 0, HALF // 2)
+                last_weight(pr, first + 1, HALF // 2, HALF // 2)
+                continue
             consume(pr, (first, first + 1))
             if k // 2 == len(pairs) - 1:
                 finish(half, slice(first, first + 2))

@@ -33,8 +33,8 @@ def tile_grconv_pa_kernel(tc, x, x_mix, WL, WR, GL, GR_bytes, GR_scale, out):
         grouped_pool = ctx.enter_context(tc.tile_pool(name="grouped_pool", bufs=3))
         codes_pool = ctx.enter_context(tc.tile_pool(name="codes_pool", bufs=6))
         mix_pool = ctx.enter_context(tc.tile_pool(name="mix_pool", bufs=2))
-        turn_psum = ctx.enter_context(tc.psum_pool(name="turn_psum", bufs=4))
-        plane_psum = ctx.enter_context(tc.psum_pool(name="plane_psum", bufs=4))
+        turn_psum = ctx.enter_context(tc.psum_pool(name="turn_psum", bufs=5))
+        plane_psum = ctx.enter_context(tc.psum_pool(name="plane_psum", bufs=3))
 
         x_view = x.rearrange("s a b k -> (a b) s k")
         mix_view = x_mix.rearrange("s a b h -> (a b) s h")

@@ -91,7 +91,7 @@ def tile_grconv_pa_kernel(tc, x, x_mix, WL, WR, GL, GR_bytes, GR_scale, out):
         rows_to_load = [x_first, x_last] + [g for g in weight_groups if not g["from_bytes"]]
         bytes_to_load = [g for g in weight_groups if g["from_bytes"]]
         piecewise = (x_first["name"], pairs[0][2]["name"], pairs[0][3]["name"])
-        mix_follows = pairs[2][2]["name"]
+        mix_follows = pairs[3][2]["name"]
 
         def load(dst, g):
             if g["name"] in piecewise:

@@ -20,7 +20,26 @@ HALF = 512
 TILES = 4
 POSITIONS = 4
 
-PAIR_ORDER = (("g1", 0), ("zc", 0), ("g0", 0), ("g1", 1), ("g0", 1), ("g2", 0), ("zc", 1), ("g2", 1))
+PAIR_ORDER = (("g1",0),("g0",0),("g1",1),("g0",1),("g2",0),("zc",0),("zc",1),("g2",1))
+LEAD = 7
+GRAIN = 2
+WIDEN_AHEAD = 3
+WIDEN_TILES = 2
+QUANT_AFTER = 1.2
+MULT = 0.5
+SCALAR_AFTER = 0.55
+VECTOR_AFTER = 0.52
+SECOND_AFTER = 0.6
+LN_AFTER = 0.7
+DIFF_AFTER = 1.5
+DIFF_STEP = 0.02
+MU_AFTER, MU_PIECE = 3, 4
+DR_AFTER, DR_PIECE = 1, 4
+CD_AFTER, CD_PIECE = 1, 2
+FIN_AFTER, FIN_PIECE = 0.6, 4
+EARLY_WIDE, EARLY_WIDE2 = 6, 8
+XQ1, XQ2 = -900, -899.6
+QPARTS = 2
 
 
 def tile_grconv_pa_kernel(tc, x, x_mix, WL, WR, GL, GR_bytes, GR_scale, out):
@@ -29,8 +48,8 @@ def tile_grconv_pa_kernel(tc, x, x_mix, WL, WR, GL, GR_bytes, GR_scale, out):
         const = ctx.enter_context(tc.tile_pool(name="const", bufs=1))
         rows_pool = ctx.enter_context(tc.tile_pool(name="rows_pool", bufs=4))
         bytes_pool = ctx.enter_context(tc.tile_pool(name="bytes_pool", bufs=4))
-        wide_pool = ctx.enter_context(tc.tile_pool(name="wide_pool", bufs=3))
-        grouped_pool = ctx.enter_context(tc.tile_pool(name="grouped_pool", bufs=3))
+        wide_pool = ctx.enter_context(tc.tile_pool(name="wide_pool", bufs=2))
+        grouped_pool = ctx.enter_context(tc.tile_pool(name="grouped_pool", bufs=4 * QPARTS))
         codes_pool = ctx.enter_context(tc.tile_pool(name="codes_pool", bufs=6))
         mix_pool = ctx.enter_context(tc.tile_pool(name="mix_pool", bufs=2))
         turn_psum = ctx.enter_context(tc.psum_pool(name="turn_psum", bufs=5))
@@ -118,81 +137,87 @@ def tile_grconv_pa_kernel(tc, x, x_mix, WL, WR, GL, GR_bytes, GR_scale, out):
             load(gr_bytes, g)
             g["gr_bytes"] = gr_bytes
 
-        def widen(g):
-            wide = wide_pool.tile([P, TILES, K], BF16, name="wide", tag="wide")
-            step = 1 if g["name"] in piecewise else 2
-            for i in range(0, TILES, step):
-                nc.vector.tensor_tensor(
-                    out=wide[:, i : i + step, :],
-                    in0=g["gr_bytes"][:, i : i + step, :].bitcast(FP8),
-                    in1=scales[:, 0:step, :],
-                    op=ALU.mult,
-                )
-            g["rows"] = wide
-            load_next_bytes()
+        def widen(g, t, n):
+            if t == 0:
+                wide = wide_pool.tile([P, TILES, K], BF16, name="wide", tag="wide")
+                g["rows"] = wide
+            nc.vector.tensor_tensor(
+                out=g["rows"][:, t : t + n, :],
+                in0=g["gr_bytes"][:, t : t + n, :].bitcast(FP8),
+                in1=scales[:, 0:n, :],
+                op=ALU.mult,
+            )
+            if t + n == TILES:
+                load_next_bytes()
 
-        def turn(g):
-            n = g["tiles"]
-            grouped = grouped_pool.tile([P, n * K], BF16, name="grouped", tag="grouped", align_bytes=64)
-            grouped_words = grouped[:].bitcast(F32).rearrange("p (g i r u) -> p g i r u", g=2, i=n, u=2)
-            for i in range(n):
-                words = g["rows"][:, i, :].bitcast(F32)
-                bank = turn_psum.tile([P, 512], F32, name="bank", tag="bank")
-                for g2 in range(2):
-                    for u in range(2):
-                        c = 2 * g2 + u
-                        nc.tensor.transpose(
-                            bank[:, c * P : (c + 1) * P],
-                            words[:, 256 * g2 + u : 256 * (g2 + 1) : 2],
-                            ident_f32[:],
-                        )
-                nc.scalar.copy(
-                    out=grouped_words[:, :, i, :, :],
-                    in_=bank[:].rearrange("p (g u r) -> p g r u", g=2, u=2),
-                )
-            if not g["from_bytes"]:
+        def part_tiles(g):
+            return g["tiles"] if g["tiles"] == 1 else g["tiles"] // QPARTS
+
+        def turn(g, i):
+            n = part_tiles(g)
+            j = i % n
+            if j == 0:
+                grouped = grouped_pool.tile([P, n * K], BF16, name="grouped", tag="grouped", align_bytes=64)
+                g["grouped"] = g.get("grouped", []) + [grouped]
+            grouped_words = g["grouped"][i // n][:].bitcast(F32).rearrange("p (g i r u) -> p g i r u", g=2, i=n, u=2)
+            words = g["rows"][:, i, :].bitcast(F32)
+            bank = turn_psum.tile([P, 512], F32, name="bank", tag="bank")
+            for g2 in range(2):
+                for u in range(2):
+                    c = 2 * g2 + u
+                    nc.tensor.transpose(
+                        bank[:, c * P : (c + 1) * P],
+                        words[:, 256 * g2 + u : 256 * (g2 + 1) : 2],
+                        ident_f32[:],
+                    )
+            nc.scalar.copy(
+                out=grouped_words[:, :, j, :, :],
+                in_=bank[:].rearrange("p (g u r) -> p g r u", g=2, u=2),
+            )
+            if i == g["tiles"] - 1 and not g["from_bytes"]:
                 load_next_rows()
-            g["grouped"] = grouped
 
-        def quantise(g, pool):
-            n = g["tiles"]
-            if pool is const:
-                codes = pool.tile([P, n * 256], U32, name="codes_" + g["name"], align_bytes=64)
-                blocks = pool.tile([P, n * 256], U8, name="blocks_" + g["name"], align_bytes=64)
-            else:
-                codes = pool.tile([P, n * 256], U32, name="codes", tag="codes", align_bytes=64)
-                blocks = pool.tile([P, n * 256], U8, name="blocks", tag="blocks", align_bytes=64)
-            nc.vector.quantize_mx(out=codes[:].bitcast(FP8X4), scales=blocks[:], in_=g["grouped"][:])
-            g["codes"] = codes
-            g["blocks"] = blocks
-
-        def prepare(g, pool):
-            if g["from_bytes"]:
-                widen(g)
-            turn(g)
-            quantise(g, pool)
+        def quantise(g, part):
+            n = part_tiles(g)
+            if part == 0:
+                if g["name"][0] == "x":
+                    g["codes"] = const.tile([P, g["tiles"] * 256], U32, name="codes_" + g["name"], align_bytes=64)
+                    g["blocks"] = const.tile([P, g["tiles"] * 256], U8, name="blocks_" + g["name"], align_bytes=64)
+                else:
+                    codes = codes_pool.tile([P, g["tiles"] * 256], U32, name="codes", tag="codes", align_bytes=64)
+                    blocks = codes_pool.tile([P, g["tiles"] * 256], U8, name="blocks", tag="blocks", align_bytes=64)
+                    g["codes"] = codes
+                    g["blocks"] = blocks
+            cols = slice(part * n * 256, (part + 1) * n * 256)
+            nc.vector.quantize_mx(
+                out=g["codes"][:, cols].bitcast(FP8X4), scales=g["blocks"][:, cols], in_=g["grouped"][part][:]
+            )
 
         def x_operand(pos, g2):
             if pos < 4:
-                lo = g2 * 512 + pos * P
+                n = part_tiles(x_first)
+                lo = (pos // n) * n * 256 + g2 * n * P + (pos % n) * P
                 return x_first["codes"][:, lo : lo + P], x_first["blocks"][:, lo : lo + P]
             lo = g2 * P
             return x_last["codes"][:, lo : lo + P], x_last["blocks"][:, lo : lo + P]
 
-        def plane(s, left_group, right_group, lo=0, width=HALF):
-            acc = plane_psum.tile([P, width], F32, name="acc", tag="acc")
+        def plane(s, left_group, right_group):
+            acc = plane_psum.tile([P, HALF], F32, name="acc", tag="acc")
             passes = [(s, 0, left_group), (s, 1, left_group), (s + 1, 0, right_group), (s + 1, 1, right_group)]
-            for n, (pos, g2, grp) in enumerate(passes):
-                x_codes, x_blocks = x_operand(pos, g2)
-                nc.tensor.matmul_mx(
-                    out=acc[:],
-                    lhsT=x_codes.bitcast(FP8X4),
-                    lhsT_scale=x_blocks,
-                    rhs=grp["codes"][:, g2 * HALF + lo : g2 * HALF + lo + width].bitcast(FP8X4),
-                    rhs_scale=grp["blocks"][:, g2 * HALF + lo : g2 * HALF + lo + width],
-                    start=(n == 0),
-                    stop=(n == 3),
-                )
+            width = HALF // QPARTS
+            for part in range(QPARTS):
+                for n, (pos, g2, grp) in enumerate(passes):
+                    x_codes, x_blocks = x_operand(pos, g2)
+                    lo = part * 2 * width + g2 * width
+                    nc.tensor.matmul_mx(
+                        out=acc[:, part * width : (part + 1) * width],
+                        lhsT=x_codes.bitcast(FP8X4),
+                        lhsT_scale=x_blocks,
+                        rhs=grp["codes"][:, lo : lo + width].bitcast(FP8X4),
+                        rhs_scale=grp["blocks"][:, lo : lo + width],
+                        start=(n == 0),
+                        stop=(n == 3),
+                    )
             return acc
 
         mix = {}
@@ -201,9 +226,11 @@ def tile_grconv_pa_kernel(tc, x, x_mix, WL, WR, GL, GR_bytes, GR_scale, out):
             t = mix_pool.tile([P, POSITIONS, HALF], F32, name=name, tag=name)
             mix[(name, half)] = t
 
-        def consume(pr, positions):
-            kind, half, left_group, right_group = pr
-            if positions[0] == 0:
+        accs = {}
+
+        def multiply(pr, s):
+            kind, half = pr[0], pr[1]
+            if s == 0:
                 if kind == "zc":
                     mix_tile("c", half)
                 elif kind == "g1":
@@ -212,56 +239,64 @@ def tile_grconv_pa_kernel(tc, x, x_mix, WL, WR, GL, GR_bytes, GR_scale, out):
                     mix_tile("u", half)
                     mix_tile("d", half)
                     mix_tile("m", half)
-            for s in positions:
-                acc = plane(s, left_group, right_group)
-                if kind == "zc":
-                    nc.scalar.activation(out=mix[("c", half)][:, s, :], in_=acc[:], func=ACT.Sigmoid)
-                elif kind == "g1":
-                    nc.scalar.copy(out=mix[("g1", half)][:, s, :], in_=acc[:])
-                elif kind == "g0":
-                    g1, d, m, u = mix[("g1", half)], mix[("d", half)], mix[("m", half)], mix[("u", half)]
-                    nc.vector.tensor_tensor(out=d[:, s, :], in0=acc[:], in1=g1[:, s, :], op=ALU.subtract)
-                    nc.vector.tensor_tensor(out=m[:, s, :], in0=acc[:], in1=g1[:, s, :], op=ALU.max)
-                    nc.scalar.activation(out=d[:, s, :], in_=d[:, s, :], func=ACT.Sigmoid)
-                    nc.scalar.activation(out=u[:, s, :], in_=d[:, s, :], func=ACT.Abs, bias=-0.5)
-                else:
-                    m = mix[("m", half)]
-                    nc.vector.tensor_tensor(out=m[:, s, :], in0=acc[:], in1=m[:, s, :], op=ALU.subtract)
-                    nc.scalar.activation(out=m[:, s, :], in_=m[:, s, :], func=ACT.Sigmoid)
+            accs[(kind, half, s)] = plane(s, pr[2], pr[3])
 
-        def in_place(name, half, op, other, sl):
-            t = mix[(name, half)]
-            nc.vector.tensor_tensor(out=t[:, sl, :], in0=t[:, sl, :], in1=other, op=op)
+        def tt(out_ap, in0, in1, op):
+            nc.vector.tensor_tensor(out=out_ap, in0=in0, in1=in1, op=op)
 
-        EVERY = slice(0, POSITIONS)
+        def first_scalar(kind, half, s):
+            acc = accs[(kind, half, s)]
+            if kind == "zc":
+                nc.scalar.activation(out=mix[("c", half)][:, s, :], in_=acc[:], func=ACT.Sigmoid)
+            else:
+                nc.scalar.copy(out=mix[("g1", half)][:, s, :], in_=acc[:])
 
-        def after_g0(half):
-            cols = slice(half * HALF, (half + 1) * HALF)
-            u, d = mix[("u", half)], mix[("d", half)]
-            nc.scalar.activation(out=u[:], in_=u[:], func=ACT.Ln, bias=0.5)
-            for s in range(POSITIONS):
-                diff = plane_psum.tile([P, HALF], F32, name="acc", tag="acc")
-                nc.tensor.matmul(diff[:], lhsT=ident_bf16[:], rhs=mix_rows[:, s, cols], start=True, stop=False)
-                nc.tensor.matmul(diff[:], lhsT=minus_ident[:], rhs=mix_rows[:, s + 1, cols], start=False, stop=True)
-                nc.vector.tensor_tensor(out=d[:, s, :], in0=d[:, s, :], in1=diff[:], op=ALU.mult)
-            in_place("m", half, ALU.subtract, u[:], EVERY)
-            in_place("d", half, ALU.add, mix_rows[:, 1 : POSITIONS + 1, cols], EVERY)
-
-        def finish(half, sl, lo=0, width=HALF):
-            c, m, d = mix[("c", half)], mix[("m", half)], mix[("d", half)]
-            cols = slice(lo, lo + width)
-            nc.vector.tensor_tensor(out=c[:, sl, cols], in0=c[:, sl, cols], in1=m[:, sl, cols], op=ALU.mult)
-            nc.vector.tensor_tensor(out=c[:, sl, cols], in0=c[:, sl, cols], in1=d[:, sl, cols], op=ALU.add)
-            nc.sync.dma_start(out=out_view[:, sl, half * HALF + lo : half * HALF + lo + width], in_=c[:, sl, cols])
-
-        def last_weight(pr, s, lo, width):
-            kind, half, left_group, right_group = pr
-            acc = plane(s, left_group, right_group, lo, width)
+        def first_vector(kind, half, s):
+            acc = accs[(kind, half, s)]
             m = mix[("m", half)]
-            cols = slice(lo, lo + width)
-            nc.vector.tensor_tensor(out=m[:, s, cols], in0=acc[:], in1=m[:, s, cols], op=ALU.subtract)
-            nc.scalar.activation(out=m[:, s, cols], in_=m[:, s, cols], func=ACT.Sigmoid)
-            finish(half, slice(s, s + 1), lo, width)
+            if kind == "g0":
+                g1, d = mix[("g1", half)], mix[("d", half)]
+                tt(d[:, s, :], acc[:], g1[:, s, :], ALU.subtract)
+                tt(m[:, s, :], acc[:], g1[:, s, :], ALU.max)
+            else:
+                tt(m[:, s, :], acc[:], m[:, s, :], ALU.subtract)
+
+        def second_scalar(kind, half, s):
+            if kind == "g0":
+                d, u = mix[("d", half)], mix[("u", half)]
+                nc.scalar.activation(out=d[:, s, :], in_=d[:, s, :], func=ACT.Sigmoid)
+                nc.scalar.activation(out=u[:, s, :], in_=d[:, s, :], func=ACT.Abs, bias=-0.5)
+            else:
+                m = mix[("m", half)]
+                nc.scalar.activation(out=m[:, s, :], in_=m[:, s, :], func=ACT.Sigmoid)
+
+        def logarithm(half):
+            u = mix[("u", half)]
+            nc.scalar.activation(out=u[:], in_=u[:], func=ACT.Ln, bias=0.5)
+
+        diffs = {}
+
+        def difference(half, s):
+            cols = slice(half * HALF, (half + 1) * HALF)
+            diff = plane_psum.tile([P, HALF], F32, name="acc", tag="acc")
+            nc.tensor.matmul(diff[:], lhsT=ident_bf16[:], rhs=mix_rows[:, s, cols], start=True, stop=False)
+            nc.tensor.matmul(diff[:], lhsT=minus_ident[:], rhs=mix_rows[:, s + 1, cols], start=False, stop=True)
+            diffs[(half, s)] = diff
+
+        def scale_difference(half, s):
+            d = mix[("d", half)]
+            tt(d[:, s, :], d[:, s, :], diffs[(half, s)][:], ALU.mult)
+
+        def in_place(name, half, op, other, lo, hi):
+            t = mix[(name, half)]
+            if other == "right":
+                operand = mix_rows[:, lo + 1 : hi + 1, half * HALF : (half + 1) * HALF]
+            else:
+                operand = mix[(other, half)][:, lo:hi, :]
+            tt(t[:, lo:hi, :], t[:, lo:hi, :], operand, op)
+
+        def store(half, lo, hi):
+            nc.sync.dma_start(out=out_view[:, lo:hi, half * HALF : (half + 1) * HALF], in_=mix[("c", half)][:, lo:hi, :])
 
         load_next_bytes()
         load_next_bytes()
@@ -270,34 +305,82 @@ def tile_grconv_pa_kernel(tc, x, x_mix, WL, WR, GL, GR_bytes, GR_scale, out):
         for n in range(2):
             load_next_bytes()
 
-        prepare(x_first, const)
-        prepare(x_last, const)
-        prepare(weight_groups[0], codes_pool)
-        prepare(weight_groups[1], codes_pool)
+        events = []
 
-        steps = 2 * len(pairs)
-        seen = set()
-        for k in range(steps):
-            pr = pairs[k // 2]
-            kind, half = pr[0], pr[1]
-            first = 2 * (k % 2)
-            if k + 2 < steps:
-                prepare(weight_groups[k + 2], codes_pool)
-            if k == steps - 1:
-                last_weight(pr, first, 0, HALF)
-                last_weight(pr, first + 1, 0, HALF // 2)
-                last_weight(pr, first + 1, HALF // 2, HALF // 2)
-                continue
-            consume(pr, (first, first + 1))
-            if k // 2 == len(pairs) - 1:
-                finish(half, slice(first, first + 2))
-                continue
-            if first == 0:
-                continue
-            seen.add((kind, half))
-            if kind == "g0":
-                after_g0(half)
-            if kind in ("g0", "zc") and ("g0", half) in seen and ("zc", half) in seen:
-                in_place("c", half, ALU.subtract, mix[("d", half)][:], EVERY)
-            if kind in ("g2", "zc") and ("g2", half) in seen and ("zc", half) in seen:
-                finish(half, EVERY)
+        def at(key, fn, *args):
+            events.append((key, len(events), fn, args))
+
+        def turn_key(i):
+            return (i // GRAIN) * GRAIN / 2 - LEAD
+
+        for i in range(4):
+            at(-1000 + i, turn, x_first, i)
+        at(-990, turn, x_last, 0)
+        for part in range(QPARTS):
+            at(XQ1 + 0.01 * part, quantise, x_first, part)
+        at(XQ2, quantise, x_last, 0)
+        wide_count = 0
+        for gi, g in enumerate(weight_groups):
+            for t in range(TILES):
+                at(turn_key(4 * gi + t) + 0.001 * t, turn, g, t)
+            if g["from_bytes"]:
+                for t in range(0, TILES, 1 if g["name"] in piecewise else WIDEN_TILES):
+                    key = turn_key(4 * gi + t) - WIDEN_AHEAD
+                    if wide_count < EARLY_WIDE:
+                        key = -1100 + wide_count
+                    elif wide_count < EARLY_WIDE2:
+                        key = -890 + wide_count
+                    n = 1 if g["name"] in piecewise else WIDEN_TILES
+                    wide_count += n
+                    at(key, widen, g, t, n)
+            for part in range(QPARTS):
+                last = (part + 1) * TILES // QPARTS - 1
+                at(turn_key(4 * gi + last) + QUANT_AFTER, quantise, g, part)
+
+        slot = {}
+        for pi, pr in enumerate(pairs):
+            for s in range(POSITIONS):
+                kind, half, m = pr[0], pr[1], 4 * pi + s
+                slot[(kind, half, s)] = m
+                at(m + MULT, multiply, pr, s)
+                if kind in ("zc", "g1"):
+                    at(m + SCALAR_AFTER, first_scalar, kind, half, s)
+                else:
+                    at(m + VECTOR_AFTER, first_vector, kind, half, s)
+                    at(m + VECTOR_AFTER + SECOND_AFTER, second_scalar, kind, half, s)
+
+        for half in range(2):
+            g0_last = slot[("g0", half, 3)]
+            at(g0_last + VECTOR_AFTER + SECOND_AFTER + LN_AFTER, logarithm, half)
+            dm_key = {}
+            for s in range(POSITIONS):
+                key = g0_last + DIFF_AFTER + DIFF_STEP * s
+                at(key, difference, half, s)
+                at(key + 0.15, scale_difference, half, s)
+                dm_key[s] = key + 0.15
+            for lo in range(0, POSITIONS, MU_PIECE):
+                at(g0_last + MU_AFTER + 0.4 * lo, in_place, "m", half, ALU.subtract, "u", lo, lo + MU_PIECE)
+            dr_key = {}
+            for lo in range(0, POSITIONS, DR_PIECE):
+                key = max(dm_key[lo + DR_PIECE - 1] + 0.05, g0_last + DR_AFTER + 0.4 * lo)
+                for s in range(lo, lo + DR_PIECE):
+                    dr_key[s] = key
+                at(key, in_place, "d", half, ALU.add, "right", lo, lo + DR_PIECE)
+            cd_key = {}
+            for lo in range(0, POSITIONS, CD_PIECE):
+                hi = lo + CD_PIECE
+                key = max(dr_key[hi - 1], slot[("zc", half, hi - 1)] + SCALAR_AFTER) + CD_AFTER
+                for s in range(lo, hi):
+                    cd_key[s] = key
+                at(key, in_place, "c", half, ALU.subtract, "d", lo, hi)
+            piece = 1 if half == pairs[-1][1] else FIN_PIECE
+            for lo in range(0, POSITIONS, piece):
+                hi = lo + piece
+                key = max(cd_key[hi - 1], slot[("g2", half, hi - 1)] + VECTOR_AFTER + SECOND_AFTER) + FIN_AFTER
+                at(key, in_place, "c", half, ALU.mult, "m", lo, hi)
+                at(key + 0.1, in_place, "c", half, ALU.add, "d", lo, hi)
+                at(key + 0.1, store, half, lo, hi)
+
+        with tc.manual_schedule():
+            for key, n, fn, args in sorted(events, key=lambda e: (e[0], e[1])):
+                fn(*args)

@@ -28,18 +28,18 @@ WIDEN_TILES = 2
 QUANT_AFTER = 1.2
 MULT = 0.5
 SCALAR_AFTER = 0.55
-VECTOR_AFTER = 0.52
+VECTOR_AFTER = 1.1
 SECOND_AFTER = 0.6
-LN_AFTER = 0.7
+LN_AFTER = 0.05
 DIFF_AFTER = 1.5
 DIFF_STEP = 0.02
-MU_AFTER, MU_PIECE = 3, 4
-DR_AFTER, DR_PIECE = 1, 4
-CD_AFTER, CD_PIECE = 1, 2
-FIN_AFTER, FIN_PIECE = 0.6, 4
+MU_AFTER, MU_PIECE = 4, 4
+DR_AFTER, DR_PIECE = 1, 2
+CD_AFTER, CD_PIECE = 1, 1
+FIN_AFTER, FIN_PIECE = 2, 2
 EARLY_WIDE, EARLY_WIDE2 = 6, 8
 XQ1, XQ2 = -900, -899.6
-QPARTS = 2
+QPARTS = 1
 
 
 def tile_grconv_pa_kernel(tc, x, x_mix, WL, WR, GL, GR_bytes, GR_scale, out):

@@ -70,8 +70,24 @@ def tile_grconv_pa_kernel(tc, x, x_mix, WL, WR, GL, GR_bytes, GR_scale, out):
         table_warm = const.tile([P, 1], F32, name="table_warm")
         nc.scalar.activation(out=table_warm[:], in_=zero_col[:], func=ACT.Sigmoid)
 
+        seeds = const.tile([P, 8], F32, name="seeds")
+        nc.sync.dma_start(
+            out=seeds[:].rearrange("p (h j) -> p h j", j=4),
+            in_=GR_scale.rearrange("o (h p j) -> (o p) h j", h=2, j=4),
+        )
         scales = const.tile([P, 2, K], F32, name="scales")
-        nc.sync.dma_start(out=scales[:, 0, :], in_=GR_scale.rearrange("o k -> (o k)").partition_broadcast(P))
+        seed_banks = []
+        for h in range(2):
+            seed_bank = turn_psum.tile([P, 512], F32, name="bank", tag="bank")
+            for j in range(4):
+                nc.tensor.transpose(
+                    seed_bank[:, j * P : (j + 1) * P],
+                    seeds[:, 4 * h + j : 4 * h + j + 1].to_broadcast([P, P]),
+                    ident_f32[:],
+                )
+            seed_banks.append(seed_bank[:].rearrange("p (j n) -> p n j", j=4))
+        nc.scalar.copy(out=scales[:, 0, 0:512], in_=seed_banks[0])
+        nc.vector.tensor_copy(out=scales[:, 0, 512:K], in_=seed_banks[1])
         nc.scalar.copy(out=scales[:, 1, :], in_=scales[:, 0, :])
         mix_rows = const.tile([P, POSITIONS + 1, K], BF16, name="mix_rows")
 

@@ -20,26 +20,9 @@ HALF = 512
 TILES = 4
 POSITIONS = 4
 
-PAIR_ORDER = (("g1",0),("g0",0),("g1",1),("g0",1),("g2",0),("zc",0),("zc",1),("g2",1))
-LEAD = 7
-GRAIN = 2
-WIDEN_AHEAD = 3
-WIDEN_TILES = 2
-QUANT_AFTER = 1.2
-MULT = 0.5
-SCALAR_AFTER = 0.55
-VECTOR_AFTER = 1.1
-SECOND_AFTER = 0.6
-LN_AFTER = 0.05
-DIFF_AFTER = 1.5
-DIFF_STEP = 0.02
-MU_AFTER, MU_PIECE = 4, 4
-DR_AFTER, DR_PIECE = 1, 2
-CD_AFTER, CD_PIECE = 1, 1
-FIN_AFTER, FIN_PIECE = 2, 2
-EARLY_WIDE, EARLY_WIDE2 = 6, 8
-XQ1, XQ2 = -900, -899.6
-QPARTS = 1
+MINUS_HALVES = ()
+ORDER_OF_PAIRS = (("g1",0),("g0",0),("g1",1),("g0",1),("zc",0),("g2",0),("zc",1),("g2",1))
+TUNE = {"lead": 11, "rho": 0.5, "gT": 1, "wl": 3, "gW": 2, "ql": 1.6, "ps": 0.1, "abl": 1, "l1": 0.7, "dk": 2, "ds": 0.02, "mul": 3, "mup": 4, "drl": 3, "drp": 4, "zl": 0.3, "szl": 0.1, "ck": 3, "cdp": 2, "fk": 1.2, "fp": 2, "ne": 4, "ne2": 12, "xq": -885.5, "mixpair": 4, "nfirst": 0, "aw": 2}
 
 
 def tile_grconv_pa_kernel(tc, x, x_mix, WL, WR, GL, GR_bytes, GR_scale, out):
@@ -49,9 +32,11 @@ def tile_grconv_pa_kernel(tc, x, x_mix, WL, WR, GL, GR_bytes, GR_scale, out):
         rows_pool = ctx.enter_context(tc.tile_pool(name="rows_pool", bufs=4))
         bytes_pool = ctx.enter_context(tc.tile_pool(name="bytes_pool", bufs=4))
         wide_pool = ctx.enter_context(tc.tile_pool(name="wide_pool", bufs=2))
-        grouped_pool = ctx.enter_context(tc.tile_pool(name="grouped_pool", bufs=4 * QPARTS))
+        grouped_pool = ctx.enter_context(tc.tile_pool(name="grouped_pool", bufs=4))
         codes_pool = ctx.enter_context(tc.tile_pool(name="codes_pool", bufs=6))
+        neg_pool = ctx.enter_context(tc.tile_pool(name="neg_pool", bufs=2))
         mix_pool = ctx.enter_context(tc.tile_pool(name="mix_pool", bufs=2))
+        log_pool = ctx.enter_context(tc.tile_pool(name="log_pool", bufs=1))
         turn_psum = ctx.enter_context(tc.psum_pool(name="turn_psum", bufs=5))
         plane_psum = ctx.enter_context(tc.psum_pool(name="plane_psum", bufs=3))
 
@@ -86,9 +71,8 @@ def tile_grconv_pa_kernel(tc, x, x_mix, WL, WR, GL, GR_bytes, GR_scale, out):
                     ident_f32[:],
                 )
             seed_banks.append(seed_bank[:].rearrange("p (j n) -> p n j", j=4))
-        nc.scalar.copy(out=scales[:, 0, 0:512], in_=seed_banks[0])
-        nc.vector.tensor_copy(out=scales[:, 0, 512:K], in_=seed_banks[1])
-        nc.scalar.copy(out=scales[:, 1, :], in_=scales[:, 0, :])
+        nc.vector.tensor_copy(out=scales[:, 0, 0:512], in_=seed_banks[0])
+        nc.scalar.copy(out=scales[:, 0, 512:K], in_=seed_banks[1])
         mix_rows = const.tile([P, POSITIONS + 1, K], BF16, name="mix_rows")
 
         def weight_group(name, dram, first_row, from_bytes):
@@ -97,10 +81,11 @@ def tile_grconv_pa_kernel(tc, x, x_mix, WL, WR, GL, GR_bytes, GR_scale, out):
                 "src": dram[first_row : first_row + HALF, :].rearrange("(i p) k -> p i k", p=P),
                 "from_bytes": from_bytes,
                 "tiles": TILES,
+                "minus": name[:4] in ("gl_n", "gr_n"),
             }
 
-        x_first = {"name": "x_first", "src": x_view[:, 0:4, :], "from_bytes": False, "tiles": 4}
-        x_last = {"name": "x_last", "src": x_view[:, 4:5, :], "from_bytes": False, "tiles": 1}
+        x_first = {"name": "x_first", "src": x_view[:, 0:4, :], "from_bytes": False, "tiles": 4, "minus": False}
+        x_last = {"name": "x_last", "src": x_view[:, 4:5, :], "from_bytes": False, "tiles": 1, "minus": False}
 
         def make_pair(kind, half):
             if kind == "zc":
@@ -119,14 +104,14 @@ def tile_grconv_pa_kernel(tc, x, x_mix, WL, WR, GL, GR_bytes, GR_scale, out):
                 weight_group("gr_%s_%d" % (kind, half), GR_bytes, first_row, True),
             )
 
-        pairs = [make_pair(kind, half) for kind, half in PAIR_ORDER]
+        pairs = [make_pair(kind, half) for kind, half in ORDER_OF_PAIRS]
         weight_groups = []
         for pr in pairs:
             weight_groups.extend([pr[2], pr[3]])
         rows_to_load = [x_first, x_last] + [g for g in weight_groups if not g["from_bytes"]]
         bytes_to_load = [g for g in weight_groups if g["from_bytes"]]
         piecewise = (x_first["name"], pairs[0][2]["name"], pairs[0][3]["name"])
-        mix_follows = pairs[3][2]["name"]
+        mix_follows = pairs[TUNE["mixpair"]][2]["name"]
 
         def load(dst, g):
             if g["name"] in piecewise:
@@ -157,25 +142,21 @@ def tile_grconv_pa_kernel(tc, x, x_mix, WL, WR, GL, GR_bytes, GR_scale, out):
             if t == 0:
                 wide = wide_pool.tile([P, TILES, K], BF16, name="wide", tag="wide")
                 g["rows"] = wide
-            nc.vector.tensor_tensor(
-                out=g["rows"][:, t : t + n, :],
-                in0=g["gr_bytes"][:, t : t + n, :].bitcast(FP8),
-                in1=scales[:, 0:n, :],
+            for lo, hi in ((0, 512), (512, K)) if t == 0 and g["name"] in piecewise else ((0, K),):
+              nc.vector.tensor_tensor(
+                out=g["rows"][:, t : t + n, lo:hi],
+                in0=g["gr_bytes"][:, t : t + n, lo:hi].bitcast(FP8),
+                in1=scales[:, 0:n, lo:hi],
                 op=ALU.mult,
-            )
+              )
             if t + n == TILES:
                 load_next_bytes()
 
-        def part_tiles(g):
-            return g["tiles"] if g["tiles"] == 1 else g["tiles"] // QPARTS
-
         def turn(g, i):
-            n = part_tiles(g)
-            j = i % n
-            if j == 0:
+            n = g["tiles"]
+            if i == 0:
                 grouped = grouped_pool.tile([P, n * K], BF16, name="grouped", tag="grouped", align_bytes=64)
-                g["grouped"] = g.get("grouped", []) + [grouped]
-            grouped_words = g["grouped"][i // n][:].bitcast(F32).rearrange("p (g i r u) -> p g i r u", g=2, i=n, u=2)
+                g["grouped"] = grouped
             words = g["rows"][:, i, :].bitcast(F32)
             bank = turn_psum.tile([P, 512], F32, name="bank", tag="bank")
             for g2 in range(2):
@@ -186,76 +167,99 @@ def tile_grconv_pa_kernel(tc, x, x_mix, WL, WR, GL, GR_bytes, GR_scale, out):
                         words[:, 256 * g2 + u : 256 * (g2 + 1) : 2],
                         ident_f32[:],
                     )
-            nc.scalar.copy(
-                out=grouped_words[:, :, j, :, :],
-                in_=bank[:].rearrange("p (g u r) -> p g r u", g=2, u=2),
-            )
-            if i == g["tiles"] - 1 and not g["from_bytes"]:
+            if g["minus"] and not g["from_bytes"]:
+                grouped_halves = g["grouped"][:].rearrange("p (g i r u e) -> p g i r u e", g=2, i=n, u=2, e=2)
+                bank_halves = bank[:].bitcast(BF16).rearrange("p (g u r e) -> p g r u e", g=2, u=2, e=2)
+                for g2 in range(2):
+                    nc.scalar.mul(out=grouped_halves[:, g2, i, :, :, :], in_=bank_halves[:, g2], mul=-1.0)
+            else:
+                grouped_words = g["grouped"][:].bitcast(F32).rearrange("p (g i r u) -> p g i r u", g=2, i=n, u=2)
+                nc.scalar.copy(
+                    out=grouped_words[:, :, i, :, :],
+                    in_=bank[:].rearrange("p (g u r) -> p g r u", g=2, u=2),
+                )
+            if i == n - 1 and not g["from_bytes"]:
                 load_next_rows()
 
-        def quantise(g, part):
-            n = part_tiles(g)
-            if part == 0:
-                if g["name"][0] == "x":
-                    g["codes"] = const.tile([P, g["tiles"] * 256], U32, name="codes_" + g["name"], align_bytes=64)
-                    g["blocks"] = const.tile([P, g["tiles"] * 256], U8, name="blocks_" + g["name"], align_bytes=64)
-                else:
-                    codes = codes_pool.tile([P, g["tiles"] * 256], U32, name="codes", tag="codes", align_bytes=64)
-                    blocks = codes_pool.tile([P, g["tiles"] * 256], U8, name="blocks", tag="blocks", align_bytes=64)
-                    g["codes"] = codes
-                    g["blocks"] = blocks
-            cols = slice(part * n * 256, (part + 1) * n * 256)
-            nc.vector.quantize_mx(
-                out=g["codes"][:, cols].bitcast(FP8X4), scales=g["blocks"][:, cols], in_=g["grouped"][part][:]
-            )
+        def quantise(g):
+            n = g["tiles"]
+            if g["name"][0] == "x":
+                codes = const.tile([P, n * 256], U32, name="codes_" + g["name"], align_bytes=64)
+                blocks = const.tile([P, n * 256], U8, name="blocks_" + g["name"], align_bytes=64)
+            elif g["minus"]:
+                codes = neg_pool.tile([P, n * 256], U32, name="ncodes", tag="ncodes", align_bytes=64)
+                blocks = neg_pool.tile([P, n * 256], U8, name="nblocks", tag="nblocks", align_bytes=64)
+            else:
+                codes = codes_pool.tile([P, n * 256], U32, name="codes", tag="codes", align_bytes=64)
+                blocks = codes_pool.tile([P, n * 256], U8, name="blocks", tag="blocks", align_bytes=64)
+            nc.vector.quantize_mx(out=codes[:].bitcast(FP8X4), scales=blocks[:], in_=g["grouped"][:])
+            g["codes"] = codes
+            g["blocks"] = blocks
 
         def x_operand(pos, g2):
             if pos < 4:
-                n = part_tiles(x_first)
-                lo = (pos // n) * n * 256 + g2 * n * P + (pos % n) * P
+                lo = g2 * 512 + pos * P
                 return x_first["codes"][:, lo : lo + P], x_first["blocks"][:, lo : lo + P]
             lo = g2 * P
             return x_last["codes"][:, lo : lo + P], x_last["blocks"][:, lo : lo + P]
 
-        def plane(s, left_group, right_group):
-            acc = plane_psum.tile([P, HALF], F32, name="acc", tag="acc")
-            passes = [(s, 0, left_group), (s, 1, left_group), (s + 1, 0, right_group), (s + 1, 1, right_group)]
-            width = HALF // QPARTS
-            for part in range(QPARTS):
-                for n, (pos, g2, grp) in enumerate(passes):
-                    x_codes, x_blocks = x_operand(pos, g2)
-                    lo = part * 2 * width + g2 * width
-                    nc.tensor.matmul_mx(
-                        out=acc[:, part * width : (part + 1) * width],
-                        lhsT=x_codes.bitcast(FP8X4),
-                        lhsT_scale=x_blocks,
-                        rhs=grp["codes"][:, lo : lo + width].bitcast(FP8X4),
-                        rhs_scale=grp["blocks"][:, lo : lo + width],
-                        start=(n == 0),
-                        stop=(n == 3),
-                    )
+        groups_of = {}
+        for pr in pairs:
+            groups_of[(pr[0], pr[1])] = (pr[2], pr[3])
+
+        def plane(kind, half, s, part=None):
+            if part == 1:
+                acc = accs[(kind, half, s)]
+            else:
+                acc = plane_psum.tile([P, HALF], F32, name="acc", tag="acc")
+            own = groups_of[(kind, half)]
+            sides = [own]
+            if kind in ("g0", "g2") and half in MINUS_HALVES:
+                sides = [groups_of[("n1", half)], own] if TUNE["nfirst"] else [own, groups_of[("n1", half)]]
+            passes = []
+            for left, right in sides:
+                passes.extend([(s, 0, left), (s, 1, left), (s + 1, 0, right), (s + 1, 1, right)])
+            for n, (pos, g2, grp) in enumerate(passes):
+                if part is not None and n // 4 != part:
+                    continue
+                x_codes, x_blocks = x_operand(pos, g2)
+                nc.tensor.matmul_mx(
+                    out=acc[:],
+                    lhsT=x_codes.bitcast(FP8X4),
+                    lhsT_scale=x_blocks,
+                    rhs=grp["codes"][:, g2 * HALF : (g2 + 1) * HALF].bitcast(FP8X4),
+                    rhs_scale=grp["blocks"][:, g2 * HALF : (g2 + 1) * HALF],
+                    start=(n == 0),
+                    stop=(n == len(passes) - 1),
+                )
             return acc
 
         mix = {}
 
         def mix_tile(name, half):
-            t = mix_pool.tile([P, POSITIONS, HALF], F32, name=name, tag=name)
-            mix[(name, half)] = t
+            if name == "g1":
+                g1 = log_pool.tile([P, POSITIONS, HALF], F32, name="g1", tag="g1")
+                mix[(name, half)] = g1
+            elif name == "u":
+                u = log_pool.tile([P, POSITIONS, HALF], F32, name="u", tag="u")
+                mix[(name, half)] = u
+            else:
+                t = mix_pool.tile([P, POSITIONS, HALF], F32, name=name, tag=name)
+                mix[(name, half)] = t
 
         accs = {}
 
-        def multiply(pr, s):
-            kind, half = pr[0], pr[1]
-            if s == 0:
+        def multiply(kind, half, s, part=None):
+            if s == 0 and part != 1:
                 if kind == "zc":
                     mix_tile("c", half)
                 elif kind == "g1":
                     mix_tile("g1", half)
                 elif kind == "g0":
-                    mix_tile("u", half)
                     mix_tile("d", half)
                     mix_tile("m", half)
-            accs[(kind, half, s)] = plane(s, pr[2], pr[3])
+                    mix_tile("u", half)
+            accs[(kind, half, s)] = plane(kind, half, s, part)
 
         def tt(out_ap, in0, in1, op):
             nc.vector.tensor_tensor(out=out_ap, in0=in0, in1=in1, op=op)
@@ -264,31 +268,37 @@ def tile_grconv_pa_kernel(tc, x, x_mix, WL, WR, GL, GR_bytes, GR_scale, out):
             acc = accs[(kind, half, s)]
             if kind == "zc":
                 nc.scalar.activation(out=mix[("c", half)][:, s, :], in_=acc[:], func=ACT.Sigmoid)
-            else:
+            elif kind == "g1":
                 nc.scalar.copy(out=mix[("g1", half)][:, s, :], in_=acc[:])
-
-        def first_vector(kind, half, s):
-            acc = accs[(kind, half, s)]
-            m = mix[("m", half)]
-            if kind == "g0":
-                g1, d = mix[("g1", half)], mix[("d", half)]
-                tt(d[:, s, :], acc[:], g1[:, s, :], ALU.subtract)
-                tt(m[:, s, :], acc[:], g1[:, s, :], ALU.max)
+            elif half not in MINUS_HALVES:
+                d, w = mix[("d", half)], 1
+                if s % w == w - 1:
+                    d_cols = d[:, s - w + 1 : s + 1, :]
+                    nc.scalar.activation(out=d_cols, in_=d_cols, func=ACT.Sigmoid)
             else:
-                tt(m[:, s, :], acc[:], m[:, s, :], ALU.subtract)
+                nc.scalar.activation(out=mix[("d", half)][:, s, :], in_=acc[:], func=ACT.Sigmoid)
+                nc.scalar.activation(out=mix[("m", half)][:, s, :], in_=acc[:], func=ACT.Relu)
 
-        def second_scalar(kind, half, s):
-            if kind == "g0":
-                d, u = mix[("d", half)], mix[("u", half)]
-                nc.scalar.activation(out=d[:, s, :], in_=d[:, s, :], func=ACT.Sigmoid)
-                nc.scalar.activation(out=u[:, s, :], in_=d[:, s, :], func=ACT.Abs, bias=-0.5)
-            else:
-                m = mix[("m", half)]
-                nc.scalar.activation(out=m[:, s, :], in_=m[:, s, :], func=ACT.Sigmoid)
+        def first_vector(half, s):
+            acc, g1 = accs[("g0", half, s)], mix[("g1", half)]
+            tt(mix[("d", half)][:, s, :], acc[:], g1[:, s, :], ALU.subtract)
+            tt(mix[("m", half)][:, s, :], acc[:], g1[:, s, :], ALU.max)
+
+        def absolute(half, lo, n):
+            d, u = mix[("d", half)], mix[("u", half)]
+            nc.scalar.activation(out=u[:, lo : lo + n, :], in_=d[:, lo : lo + n, :], func=ACT.Abs, bias=-0.5)
 
         def logarithm(half):
             u = mix[("u", half)]
             nc.scalar.activation(out=u[:], in_=u[:], func=ACT.Ln, bias=0.5)
+
+        def last_vector(half, s):
+            m = mix[("m", half)]
+            tt(m[:, s, :], accs[("g2", half, s)][:], m[:, s, :], ALU.subtract)
+
+        def last_scalar(half, s, w):
+            m = mix[("m", half)][:, s - w + 1 : s + 1, :]
+            nc.scalar.activation(out=m, in_=m, func=ACT.Sigmoid)
 
         diffs = {}
 
@@ -321,82 +331,103 @@ def tile_grconv_pa_kernel(tc, x, x_mix, WL, WR, GL, GR_bytes, GR_scale, out):
         for n in range(2):
             load_next_bytes()
 
+        def double_scales():
+            nc.scalar.copy(out=scales[:, 1, :], in_=scales[:, 0, :])
+
         events = []
 
         def at(key, fn, *args):
             events.append((key, len(events), fn, args))
 
+        T = TUNE
+
+        at(-998.5, double_scales)
+
         def turn_key(i):
-            return (i // GRAIN) * GRAIN / 2 - LEAD
+            return (i // T["gT"]) * T["gT"] * T["rho"] - T["lead"]
 
         for i in range(4):
             at(-1000 + i, turn, x_first, i)
         at(-990, turn, x_last, 0)
-        for part in range(QPARTS):
-            at(XQ1 + 0.01 * part, quantise, x_first, part)
-        at(XQ2, quantise, x_last, 0)
-        wide_count = 0
+        at(T["xq"], quantise, x_first)
+        at(T["xq"] + 0.01, quantise, x_last)
+        count = 0
         for gi, g in enumerate(weight_groups):
             for t in range(TILES):
-                at(turn_key(4 * gi + t) + 0.001 * t, turn, g, t)
+                at(turn_key(4 * gi + t) + 0.0001 * t, turn, g, t)
             if g["from_bytes"]:
-                for t in range(0, TILES, 1 if g["name"] in piecewise else WIDEN_TILES):
-                    key = turn_key(4 * gi + t) - WIDEN_AHEAD
-                    if wide_count < EARLY_WIDE:
-                        key = -1100 + wide_count
-                    elif wide_count < EARLY_WIDE2:
-                        key = -890 + wide_count
-                    n = 1 if g["name"] in piecewise else WIDEN_TILES
-                    wide_count += n
-                    at(key, widen, g, t, n)
-            for part in range(QPARTS):
-                last = (part + 1) * TILES // QPARTS - 1
-                at(turn_key(4 * gi + last) + QUANT_AFTER, quantise, g, part)
-
-        slot = {}
-        for pi, pr in enumerate(pairs):
+                width = 1 if count < 4 or g["minus"] else T["gW"]
+                for t in range(0, TILES, width):
+                    key = turn_key(4 * gi + t) - T["wl"]
+                    if count < T["ne"]:
+                        key = -1100 + count
+                    elif count < T["ne2"]:
+                        key = -890 + count
+                    count += width
+                    at(key, widen, g, t, width)
+            at(turn_key(4 * gi + 3) + T["ql"], quantise, g)
+        ends = {}
+        m = 0
+        for pr in pairs:
+            if pr[0] == "n1":
+                continue
             for s in range(POSITIONS):
-                kind, half, m = pr[0], pr[1], 4 * pi + s
-                slot[(kind, half, s)] = m
-                at(m + MULT, multiply, pr, s)
-                if kind in ("zc", "g1"):
-                    at(m + SCALAR_AFTER, first_scalar, kind, half, s)
+                if pr[0] != "zc" and pr[1] in MINUS_HALVES:
+                    at(m + 0.01, multiply, pr[0], pr[1], s, 0)
+                    at(m + 1.01, multiply, pr[0], pr[1], s, 1)
                 else:
-                    at(m + VECTOR_AFTER, first_vector, kind, half, s)
-                    at(m + VECTOR_AFTER + SECOND_AFTER, second_scalar, kind, half, s)
-
+                    at(m + 0.01, multiply, pr[0], pr[1], s)
+                m += 2 if pr[0] != "zc" and pr[1] in MINUS_HALVES else 1
+                ends[(pr[0], pr[1], s)] = m
+        for (kind, half, s), e in ends.items():
+            late = 0
+            if kind == "g0" and half not in MINUS_HALVES:
+                at(e + T["zl"], first_vector, half, s)
+                late = T["zl"]
+            if kind in ("zc", "g0", "g1"):
+                at(e + late + T["ps"], first_scalar, kind, half, s)
+            if kind == "g0" and s % T["aw"] == T["aw"] - 1:
+                at(e + late + T["ps"] + T["abl"], absolute, half, s - T["aw"] + 1, T["aw"])
+            if kind == "g2":
+                at(e + T["zl"], last_vector, half, s)
+                w = 2 if half != pairs[-1][1] else 1
+                if s % w == w - 1:
+                    at(e + T["zl"] + T["szl"], last_scalar, half, s, w)
+        last_half = pairs[-1][1]
         for half in range(2):
-            g0_last = slot[("g0", half, 3)]
-            at(g0_last + VECTOR_AFTER + SECOND_AFTER + LN_AFTER, logarithm, half)
+            g0 = ends[("g0", half, 3)]
+            g0_all = max(ends[("g0", 0, 3)], ends[("g0", 1, 3)])
+            at(g0_all + T["ps"] + T["abl"] + T["l1"] + T["zl"] + 0.001 * half, logarithm, half)
             dm_key = {}
             for s in range(POSITIONS):
-                key = g0_last + DIFF_AFTER + DIFF_STEP * s
+                key = g0 + T["dk"] + T["ds"] * s
                 at(key, difference, half, s)
                 at(key + 0.15, scale_difference, half, s)
                 dm_key[s] = key + 0.15
-            for lo in range(0, POSITIONS, MU_PIECE):
-                at(g0_last + MU_AFTER + 0.4 * lo, in_place, "m", half, ALU.subtract, "u", lo, lo + MU_PIECE)
+            for lo in range(0, POSITIONS, T["mup"]):
+                at(g0_all + T["mul"] + 0.3 * lo + 0.1 * half, in_place, "m", half, ALU.subtract, "u", lo, lo + T["mup"])
             dr_key = {}
-            for lo in range(0, POSITIONS, DR_PIECE):
-                key = max(dm_key[lo + DR_PIECE - 1] + 0.05, g0_last + DR_AFTER + 0.4 * lo)
-                for s in range(lo, lo + DR_PIECE):
+            for lo in range(0, POSITIONS, T["drp"]):
+                key = max(dm_key[lo + T["drp"] - 1] + 0.05, g0 + T["drl"] + 0.3 * lo)
+                for s in range(lo, lo + T["drp"]):
                     dr_key[s] = key
-                at(key, in_place, "d", half, ALU.add, "right", lo, lo + DR_PIECE)
+                at(key, in_place, "d", half, ALU.add, "right", lo, lo + T["drp"])
             cd_key = {}
-            for lo in range(0, POSITIONS, CD_PIECE):
-                hi = lo + CD_PIECE
-                key = max(dr_key[hi - 1], slot[("zc", half, hi - 1)] + SCALAR_AFTER) + CD_AFTER
+            piece = T["cdp"] if half != last_half or pairs[-1][0] != "zc" else 1
+            for lo in range(0, POSITIONS, piece):
+                hi = lo + piece
+                key = max(dr_key[hi - 1], ends[("zc", half, hi - 1)] + T["ps"]) + T["ck"]
                 for s in range(lo, hi):
                     cd_key[s] = key
                 at(key, in_place, "c", half, ALU.subtract, "d", lo, hi)
-            piece = 1 if half == pairs[-1][1] else FIN_PIECE
+            piece = 1 if half == last_half else T["fp"]
             for lo in range(0, POSITIONS, piece):
                 hi = lo + piece
-                key = max(cd_key[hi - 1], slot[("g2", half, hi - 1)] + VECTOR_AFTER + SECOND_AFTER) + FIN_AFTER
+                key = max(cd_key[hi - 1], ends[("g2", half, hi - 1)] + T["zl"] + T["szl"]) + T["fk"]
                 at(key, in_place, "c", half, ALU.mult, "m", lo, hi)
                 at(key + 0.1, in_place, "c", half, ALU.add, "d", lo, hi)
                 at(key + 0.1, store, half, lo, hi)
 
-        with tc.manual_schedule():
+        with tc.manual_schedule(engines={mybir.EngineType.PE}):
             for key, n, fn, args in sorted(events, key=lambda e: (e[0], e[1])):
                 fn(*args)

@@ -20,9 +20,10 @@ HALF = 512
 TILES = 4
 POSITIONS = 4
 
-MINUS_HALVES = ()
-ORDER_OF_PAIRS = (("g1",0),("g0",0),("g1",1),("g0",1),("zc",0),("g2",0),("zc",1),("g2",1))
-TUNE = {"lead": 11, "rho": 0.5, "gT": 1, "wl": 3, "gW": 2, "ql": 1.6, "ps": 0.1, "abl": 1, "l1": 0.7, "dk": 2, "ds": 0.02, "mul": 3, "mup": 4, "drl": 3, "drp": 4, "zl": 0.3, "szl": 0.1, "ck": 3, "cdp": 2, "fk": 1.2, "fp": 2, "ne": 4, "ne2": 12, "xq": -885.5, "mixpair": 4, "nfirst": 0, "aw": 2}
+PAIR_ORDER = (("g1", 0), ("g0", 0), ("g1", 1), ("g0", 1), ("zc", 0), ("g2", 0), ("zc", 1), ("g2", 1))
+
+TURNED_AHEAD = 21
+WIDENED_AHEAD = 7
 
 
 def tile_grconv_pa_kernel(tc, x, x_mix, WL, WR, GL, GR_bytes, GR_scale, out):
@@ -34,9 +35,8 @@ def tile_grconv_pa_kernel(tc, x, x_mix, WL, WR, GL, GR_bytes, GR_scale, out):
         wide_pool = ctx.enter_context(tc.tile_pool(name="wide_pool", bufs=2))
         grouped_pool = ctx.enter_context(tc.tile_pool(name="grouped_pool", bufs=4))
         codes_pool = ctx.enter_context(tc.tile_pool(name="codes_pool", bufs=6))
-        neg_pool = ctx.enter_context(tc.tile_pool(name="neg_pool", bufs=2))
         mix_pool = ctx.enter_context(tc.tile_pool(name="mix_pool", bufs=2))
-        log_pool = ctx.enter_context(tc.tile_pool(name="log_pool", bufs=1))
+        short_pool = ctx.enter_context(tc.tile_pool(name="short_pool", bufs=1))
         turn_psum = ctx.enter_context(tc.psum_pool(name="turn_psum", bufs=5))
         plane_psum = ctx.enter_context(tc.psum_pool(name="plane_psum", bufs=3))
 
@@ -81,11 +81,10 @@ def tile_grconv_pa_kernel(tc, x, x_mix, WL, WR, GL, GR_bytes, GR_scale, out):
                 "src": dram[first_row : first_row + HALF, :].rearrange("(i p) k -> p i k", p=P),
                 "from_bytes": from_bytes,
                 "tiles": TILES,
-                "minus": name[:4] in ("gl_n", "gr_n"),
             }
 
-        x_first = {"name": "x_first", "src": x_view[:, 0:4, :], "from_bytes": False, "tiles": 4, "minus": False}
-        x_last = {"name": "x_last", "src": x_view[:, 4:5, :], "from_bytes": False, "tiles": 1, "minus": False}
+        x_first = {"name": "x_first", "src": x_view[:, 0:4, :], "from_bytes": False, "tiles": 4}
+        x_last = {"name": "x_last", "src": x_view[:, 4:5, :], "from_bytes": False, "tiles": 1}
 
         def make_pair(kind, half):
             if kind == "zc":
@@ -104,14 +103,15 @@ def tile_grconv_pa_kernel(tc, x, x_mix, WL, WR, GL, GR_bytes, GR_scale, out):
                 weight_group("gr_%s_%d" % (kind, half), GR_bytes, first_row, True),
             )
 
-        pairs = [make_pair(kind, half) for kind, half in ORDER_OF_PAIRS]
+        pairs = [make_pair(kind, half) for kind, half in PAIR_ORDER]
+        last_half = PAIR_ORDER[-1][1]
         weight_groups = []
         for pr in pairs:
             weight_groups.extend([pr[2], pr[3]])
         rows_to_load = [x_first, x_last] + [g for g in weight_groups if not g["from_bytes"]]
         bytes_to_load = [g for g in weight_groups if g["from_bytes"]]
         piecewise = (x_first["name"], pairs[0][2]["name"], pairs[0][3]["name"])
-        mix_follows = pairs[TUNE["mixpair"]][2]["name"]
+        mix_follows = pairs[4][2]["name"]
 
         def load(dst, g):
             if g["name"] in piecewise:
@@ -138,25 +138,44 @@ def tile_grconv_pa_kernel(tc, x, x_mix, WL, WR, GL, GR_bytes, GR_scale, out):
             load(gr_bytes, g)
             g["gr_bytes"] = gr_bytes
 
-        def widen(g, t, n):
-            if t == 0:
-                wide = wide_pool.tile([P, TILES, K], BF16, name="wide", tag="wide")
-                g["rows"] = wide
-            for lo, hi in ((0, 512), (512, K)) if t == 0 and g["name"] in piecewise else ((0, K),):
-              nc.vector.tensor_tensor(
-                out=g["rows"][:, t : t + n, lo:hi],
-                in0=g["gr_bytes"][:, t : t + n, lo:hi].bitcast(FP8),
+        tiles_to_turn = [(g, i) for g in weight_groups for i in range(TILES)]
+        tiles_to_widen = [n for n, (g, i) in enumerate(tiles_to_turn) if g["from_bytes"]]
+
+        def product(g, i, n, lo, hi):
+            nc.vector.tensor_tensor(
+                out=g["rows"][:, i : i + n, lo:hi],
+                in0=g["gr_bytes"][:, i : i + n, lo:hi].bitcast(FP8),
                 in1=scales[:, 0:n, lo:hi],
                 op=ALU.mult,
-              )
-            if t + n == TILES:
-                load_next_bytes()
+            )
+
+        def widen_up_to(number):
+            while tiles_to_widen and tiles_to_widen[0] < number:
+                g, i = tiles_to_turn[tiles_to_widen[0]]
+                if i == 0:
+                    wide = wide_pool.tile([P, TILES, K], BF16, name="wide", tag="wide")
+                    g["rows"] = wide
+                if g["name"] not in piecewise:
+                    step = 2
+                    product(g, i, step, 0, K)
+                elif i == 0:
+                    step = 1
+                    product(g, i, step, 0, 512)
+                    product(g, i, step, 512, K)
+                else:
+                    step = 1
+                    product(g, i, step, 0, K)
+                for n in range(step):
+                    tiles_to_widen.pop(0)
+                if i + step == TILES:
+                    load_next_bytes()
 
         def turn(g, i):
             n = g["tiles"]
             if i == 0:
                 grouped = grouped_pool.tile([P, n * K], BF16, name="grouped", tag="grouped", align_bytes=64)
                 g["grouped"] = grouped
+            grouped_words = g["grouped"][:].bitcast(F32).rearrange("p (g i r u) -> p g i r u", g=2, i=n, u=2)
             words = g["rows"][:, i, :].bitcast(F32)
             bank = turn_psum.tile([P, 512], F32, name="bank", tag="bank")
             for g2 in range(2):
@@ -167,34 +186,41 @@ def tile_grconv_pa_kernel(tc, x, x_mix, WL, WR, GL, GR_bytes, GR_scale, out):
                         words[:, 256 * g2 + u : 256 * (g2 + 1) : 2],
                         ident_f32[:],
                     )
-            if g["minus"] and not g["from_bytes"]:
-                grouped_halves = g["grouped"][:].rearrange("p (g i r u e) -> p g i r u e", g=2, i=n, u=2, e=2)
-                bank_halves = bank[:].bitcast(BF16).rearrange("p (g u r e) -> p g r u e", g=2, u=2, e=2)
-                for g2 in range(2):
-                    nc.scalar.mul(out=grouped_halves[:, g2, i, :, :, :], in_=bank_halves[:, g2], mul=-1.0)
-            else:
-                grouped_words = g["grouped"][:].bitcast(F32).rearrange("p (g i r u) -> p g i r u", g=2, i=n, u=2)
-                nc.scalar.copy(
-                    out=grouped_words[:, :, i, :, :],
-                    in_=bank[:].rearrange("p (g u r) -> p g r u", g=2, u=2),
-                )
+            nc.scalar.copy(
+                out=grouped_words[:, :, i, :, :],
+                in_=bank[:].rearrange("p (g u r) -> p g r u", g=2, u=2),
+            )
             if i == n - 1 and not g["from_bytes"]:
                 load_next_rows()
 
         def quantise(g):
             n = g["tiles"]
-            if g["name"][0] == "x":
-                codes = const.tile([P, n * 256], U32, name="codes_" + g["name"], align_bytes=64)
-                blocks = const.tile([P, n * 256], U8, name="blocks_" + g["name"], align_bytes=64)
-            elif g["minus"]:
-                codes = neg_pool.tile([P, n * 256], U32, name="ncodes", tag="ncodes", align_bytes=64)
-                blocks = neg_pool.tile([P, n * 256], U8, name="nblocks", tag="nblocks", align_bytes=64)
-            else:
+            if n == TILES and g["name"] != x_first["name"]:
                 codes = codes_pool.tile([P, n * 256], U32, name="codes", tag="codes", align_bytes=64)
                 blocks = codes_pool.tile([P, n * 256], U8, name="blocks", tag="blocks", align_bytes=64)
+            else:
+                codes = const.tile([P, n * 256], U32, name="codes_" + g["name"], align_bytes=64)
+                blocks = const.tile([P, n * 256], U8, name="blocks_" + g["name"], align_bytes=64)
             nc.vector.quantize_mx(out=codes[:].bitcast(FP8X4), scales=blocks[:], in_=g["grouped"][:])
             g["codes"] = codes
             g["blocks"] = blocks
+
+        turned = [0]
+        complete = []
+
+        def turn_next(count):
+            for number in range(turned[0], min(turned[0] + count, len(tiles_to_turn))):
+                g, i = tiles_to_turn[number]
+                turn(g, i)
+                widen_up_to(number + WIDENED_AHEAD)
+                if i == TILES - 1:
+                    complete.append(g)
+            turned[0] += count
+
+        def quantise_complete(groups):
+            for g in groups:
+                quantise(g)
+                complete.pop(0)
 
         def x_operand(pos, g2):
             if pos < 4:
@@ -203,126 +229,148 @@ def tile_grconv_pa_kernel(tc, x, x_mix, WL, WR, GL, GR_bytes, GR_scale, out):
             lo = g2 * P
             return x_last["codes"][:, lo : lo + P], x_last["blocks"][:, lo : lo + P]
 
-        groups_of = {}
-        for pr in pairs:
-            groups_of[(pr[0], pr[1])] = (pr[2], pr[3])
-
-        def plane(kind, half, s, part=None):
-            if part == 1:
-                acc = accs[(kind, half, s)]
-            else:
-                acc = plane_psum.tile([P, HALF], F32, name="acc", tag="acc")
-            own = groups_of[(kind, half)]
-            sides = [own]
-            if kind in ("g0", "g2") and half in MINUS_HALVES:
-                sides = [groups_of[("n1", half)], own] if TUNE["nfirst"] else [own, groups_of[("n1", half)]]
-            passes = []
-            for left, right in sides:
-                passes.extend([(s, 0, left), (s, 1, left), (s + 1, 0, right), (s + 1, 1, right)])
+        def plane(s, left_group, right_group, lo=0, width=HALF):
+            acc = plane_psum.tile([P, width], F32, name="acc", tag="acc")
+            passes = [(s, 0, left_group), (s, 1, left_group), (s + 1, 0, right_group), (s + 1, 1, right_group)]
             for n, (pos, g2, grp) in enumerate(passes):
-                if part is not None and n // 4 != part:
-                    continue
                 x_codes, x_blocks = x_operand(pos, g2)
                 nc.tensor.matmul_mx(
                     out=acc[:],
                     lhsT=x_codes.bitcast(FP8X4),
                     lhsT_scale=x_blocks,
-                    rhs=grp["codes"][:, g2 * HALF : (g2 + 1) * HALF].bitcast(FP8X4),
-                    rhs_scale=grp["blocks"][:, g2 * HALF : (g2 + 1) * HALF],
+                    rhs=grp["codes"][:, g2 * HALF + lo : g2 * HALF + lo + width].bitcast(FP8X4),
+                    rhs_scale=grp["blocks"][:, g2 * HALF + lo : g2 * HALF + lo + width],
                     start=(n == 0),
-                    stop=(n == len(passes) - 1),
+                    stop=(n == 3),
                 )
             return acc
 
         mix = {}
 
         def mix_tile(name, half):
-            if name == "g1":
-                g1 = log_pool.tile([P, POSITIONS, HALF], F32, name="g1", tag="g1")
-                mix[(name, half)] = g1
-            elif name == "u":
-                u = log_pool.tile([P, POSITIONS, HALF], F32, name="u", tag="u")
-                mix[(name, half)] = u
-            else:
-                t = mix_pool.tile([P, POSITIONS, HALF], F32, name=name, tag=name)
-                mix[(name, half)] = t
+            pool = short_pool if name in ("g1", "u") else mix_pool
+            t = pool.tile([P, POSITIONS, HALF], F32, name=name, tag=name)
+            mix[(name, half)] = t
 
-        accs = {}
+        def columns(half):
+            return slice(half * HALF, (half + 1) * HALF)
 
-        def multiply(kind, half, s, part=None):
-            if s == 0 and part != 1:
-                if kind == "zc":
-                    mix_tile("c", half)
-                elif kind == "g1":
-                    mix_tile("g1", half)
-                elif kind == "g0":
-                    mix_tile("d", half)
-                    mix_tile("m", half)
-                    mix_tile("u", half)
-            accs[(kind, half, s)] = plane(kind, half, s, part)
+        later = []
+        before_plane = []
+        now = [0]
+        done = {}
 
-        def tt(out_ap, in0, in1, op):
+        def after(planes, step, *args):
+            later.append((now[0] + planes, step, args))
+
+        def run_later():
+            due = [e for e in later if e[0] <= now[0]]
+            while due:
+                rest = [e for e in later if e[0] > now[0]]
+                later.clear()
+                later.extend(rest)
+                for when, step, args in due:
+                    step(*args)
+                due = [e for e in later if e[0] <= now[0]]
+
+        def tensor(out_ap, in0, in1, op):
             nc.vector.tensor_tensor(out=out_ap, in0=in0, in1=in1, op=op)
 
-        def first_scalar(kind, half, s):
-            acc = accs[(kind, half, s)]
-            if kind == "zc":
-                nc.scalar.activation(out=mix[("c", half)][:, s, :], in_=acc[:], func=ACT.Sigmoid)
-            elif kind == "g1":
-                nc.scalar.copy(out=mix[("g1", half)][:, s, :], in_=acc[:])
-            elif half not in MINUS_HALVES:
-                d, w = mix[("d", half)], 1
-                if s % w == w - 1:
-                    d_cols = d[:, s - w + 1 : s + 1, :]
-                    nc.scalar.activation(out=d_cols, in_=d_cols, func=ACT.Sigmoid)
-            else:
-                nc.scalar.activation(out=mix[("d", half)][:, s, :], in_=acc[:], func=ACT.Sigmoid)
-                nc.scalar.activation(out=mix[("m", half)][:, s, :], in_=acc[:], func=ACT.Relu)
+        def share(half, s):
+            d = mix[("d", half)][:, s, :]
+            nc.scalar.activation(out=d, in_=d, func=ACT.Sigmoid)
+            if s % 2 == 1:
+                after(1, distance, half, s - 1)
 
-        def first_vector(half, s):
-            acc, g1 = accs[("g0", half, s)], mix[("g1", half)]
-            tt(mix[("d", half)][:, s, :], acc[:], g1[:, s, :], ALU.subtract)
-            tt(mix[("m", half)][:, s, :], acc[:], g1[:, s, :], ALU.max)
-
-        def absolute(half, lo, n):
-            d, u = mix[("d", half)], mix[("u", half)]
-            nc.scalar.activation(out=u[:, lo : lo + n, :], in_=d[:, lo : lo + n, :], func=ACT.Abs, bias=-0.5)
+        def distance(half, first):
+            d = mix[("d", half)][:, first : first + 2, :]
+            nc.scalar.activation(out=mix[("u", half)][:, first : first + 2, :], in_=d, func=ACT.Abs, bias=-0.5)
+            if first + 2 == POSITIONS:
+                before_plane.append((now[0] + 1, half))
+                for s in range(1, POSITIONS):
+                    after(1, difference, half, s)
+                done[("distance", half)] = True
+                if ("distance", 1 - half) in done:
+                    for h in range(2):
+                        after(1, logarithm, h)
 
         def logarithm(half):
             u = mix[("u", half)]
             nc.scalar.activation(out=u[:], in_=u[:], func=ACT.Ln, bias=0.5)
-
-        def last_vector(half, s):
-            m = mix[("m", half)]
-            tt(m[:, s, :], accs[("g2", half, s)][:], m[:, s, :], ALU.subtract)
-
-        def last_scalar(half, s, w):
-            m = mix[("m", half)][:, s - w + 1 : s + 1, :]
-            nc.scalar.activation(out=m, in_=m, func=ACT.Sigmoid)
-
-        diffs = {}
+            after(1, log_sum, half)
 
         def difference(half, s):
-            cols = slice(half * HALF, (half + 1) * HALF)
             diff = plane_psum.tile([P, HALF], F32, name="acc", tag="acc")
+            cols = columns(half)
             nc.tensor.matmul(diff[:], lhsT=ident_bf16[:], rhs=mix_rows[:, s, cols], start=True, stop=False)
             nc.tensor.matmul(diff[:], lhsT=minus_ident[:], rhs=mix_rows[:, s + 1, cols], start=False, stop=True)
-            diffs[(half, s)] = diff
+            after(0, scale_difference, half, s, diff)
 
-        def scale_difference(half, s):
+        def scale_difference(half, s, diff):
+            d = mix[("d", half)][:, s, :]
+            tensor(d, d, diff[:], ALU.mult)
+            if s == POSITIONS - 1:
+                after(1, left_right, half)
+
+        def left_right(half):
             d = mix[("d", half)]
-            tt(d[:, s, :], d[:, s, :], diffs[(half, s)][:], ALU.mult)
+            tensor(d[:], d[:], mix_rows[:, 1 : POSITIONS + 1, columns(half)], ALU.add)
 
-        def in_place(name, half, op, other, lo, hi):
-            t = mix[(name, half)]
-            if other == "right":
-                operand = mix_rows[:, lo + 1 : hi + 1, half * HALF : (half + 1) * HALF]
+        def log_sum(half):
+            m = mix[("m", half)]
+            tensor(m[:], m[:], mix[("u", half)][:], ALU.subtract)
+
+        def center_less_y(half, first):
+            c, d = [mix[(name, half)][:, first : first + 2, :] for name in ("c", "d")]
+            tensor(c, c, d, ALU.subtract)
+
+        def finish(half, first, last, lo=0, width=HALF):
+            c, m, d = [mix[(name, half)][:, first:last, lo : lo + width] for name in ("c", "m", "d")]
+            tensor(c, c, m, ALU.mult)
+            tensor(c, c, d, ALU.add)
+            column = half * HALF + lo
+            nc.sync.dma_start(out=out_view[:, first:last, column : column + width], in_=c)
+
+        def weight(half, first, last):
+            m = mix[("m", half)][:, first:last, :]
+            nc.scalar.activation(out=m, in_=m, func=ACT.Sigmoid)
+            after(1, finish, half, first, last)
+
+        def last_plane(pr, s, lo, width):
+            kind, half, left_group, right_group = pr
+            acc = plane(s, left_group, right_group, lo, width)
+            m = mix[("m", half)][:, s, lo : lo + width]
+            tensor(m, acc[:], m, ALU.subtract)
+            nc.scalar.activation(out=m, in_=m, func=ACT.Sigmoid)
+            finish(half, s, s + 1, lo, width)
+
+        def multiply(pr, s):
+            kind, half, left_group, right_group = pr
+            if s == 0:
+                for name in {"zc": ("c",), "g1": ("g1",), "g0": ("d", "m", "u"), "g2": ()}[kind]:
+                    mix_tile(name, half)
+            acc = plane(s, left_group, right_group)
+            after(1, first_step, kind, half, s, acc)
+
+        def first_step(kind, half, s, acc):
+            if kind == "zc":
+                nc.scalar.activation(out=mix[("c", half)][:, s, :], in_=acc[:], func=ACT.Sigmoid)
+                if s % 2 == 1:
+                    after(3, center_less_y, half, s - 1)
+            elif kind == "g1":
+                nc.scalar.copy(out=mix[("g1", half)][:, s, :], in_=acc[:])
+            elif kind == "g0":
+                g1, d, m = [mix[(name, half)][:, s, :] for name in ("g1", "d", "m")]
+                tensor(d, acc[:], g1, ALU.subtract)
+                tensor(m, acc[:], g1, ALU.max)
+                after(0, share, half, s)
             else:
-                operand = mix[(other, half)][:, lo:hi, :]
-            tt(t[:, lo:hi, :], t[:, lo:hi, :], operand, op)
-
-        def store(half, lo, hi):
-            nc.sync.dma_start(out=out_view[:, lo:hi, half * HALF : (half + 1) * HALF], in_=mix[("c", half)][:, lo:hi, :])
+                m = mix[("m", half)][:, s, :]
+                tensor(m, acc[:], m, ALU.subtract)
+                if half == last_half:
+                    after(0, weight, half, s, s + 1)
+                elif s % 2 == 1:
+                    after(0, weight, half, s - 1, s + 1)
 
         load_next_bytes()
         load_next_bytes()
@@ -331,103 +379,40 @@ def tile_grconv_pa_kernel(tc, x, x_mix, WL, WR, GL, GR_bytes, GR_scale, out):
         for n in range(2):
             load_next_bytes()
 
-        def double_scales():
-            nc.scalar.copy(out=scales[:, 1, :], in_=scales[:, 0, :])
-
-        events = []
-
-        def at(key, fn, *args):
-            events.append((key, len(events), fn, args))
-
-        T = TUNE
-
-        at(-998.5, double_scales)
-
-        def turn_key(i):
-            return (i // T["gT"]) * T["gT"] * T["rho"] - T["lead"]
-
-        for i in range(4):
-            at(-1000 + i, turn, x_first, i)
-        at(-990, turn, x_last, 0)
-        at(T["xq"], quantise, x_first)
-        at(T["xq"] + 0.01, quantise, x_last)
-        count = 0
-        for gi, g in enumerate(weight_groups):
-            for t in range(TILES):
-                at(turn_key(4 * gi + t) + 0.0001 * t, turn, g, t)
-            if g["from_bytes"]:
-                width = 1 if count < 4 or g["minus"] else T["gW"]
-                for t in range(0, TILES, width):
-                    key = turn_key(4 * gi + t) - T["wl"]
-                    if count < T["ne"]:
-                        key = -1100 + count
-                    elif count < T["ne2"]:
-                        key = -890 + count
-                    count += width
-                    at(key, widen, g, t, width)
-            at(turn_key(4 * gi + 3) + T["ql"], quantise, g)
-        ends = {}
-        m = 0
-        for pr in pairs:
-            if pr[0] == "n1":
-                continue
-            for s in range(POSITIONS):
-                if pr[0] != "zc" and pr[1] in MINUS_HALVES:
-                    at(m + 0.01, multiply, pr[0], pr[1], s, 0)
-                    at(m + 1.01, multiply, pr[0], pr[1], s, 1)
-                else:
-                    at(m + 0.01, multiply, pr[0], pr[1], s)
-                m += 2 if pr[0] != "zc" and pr[1] in MINUS_HALVES else 1
-                ends[(pr[0], pr[1], s)] = m
-        for (kind, half, s), e in ends.items():
-            late = 0
-            if kind == "g0" and half not in MINUS_HALVES:
-                at(e + T["zl"], first_vector, half, s)
-                late = T["zl"]
-            if kind in ("zc", "g0", "g1"):
-                at(e + late + T["ps"], first_scalar, kind, half, s)
-            if kind == "g0" and s % T["aw"] == T["aw"] - 1:
-                at(e + late + T["ps"] + T["abl"], absolute, half, s - T["aw"] + 1, T["aw"])
-            if kind == "g2":
-                at(e + T["zl"], last_vector, half, s)
-                w = 2 if half != pairs[-1][1] else 1
-                if s % w == w - 1:
-                    at(e + T["zl"] + T["szl"], last_scalar, half, s, w)
-        last_half = pairs[-1][1]
-        for half in range(2):
-            g0 = ends[("g0", half, 3)]
-            g0_all = max(ends[("g0", 0, 3)], ends[("g0", 1, 3)])
-            at(g0_all + T["ps"] + T["abl"] + T["l1"] + T["zl"] + 0.001 * half, logarithm, half)
-            dm_key = {}
-            for s in range(POSITIONS):
-                key = g0 + T["dk"] + T["ds"] * s
-                at(key, difference, half, s)
-                at(key + 0.15, scale_difference, half, s)
-                dm_key[s] = key + 0.15
-            for lo in range(0, POSITIONS, T["mup"]):
-                at(g0_all + T["mul"] + 0.3 * lo + 0.1 * half, in_place, "m", half, ALU.subtract, "u", lo, lo + T["mup"])
-            dr_key = {}
-            for lo in range(0, POSITIONS, T["drp"]):
-                key = max(dm_key[lo + T["drp"] - 1] + 0.05, g0 + T["drl"] + 0.3 * lo)
-                for s in range(lo, lo + T["drp"]):
-                    dr_key[s] = key
-                at(key, in_place, "d", half, ALU.add, "right", lo, lo + T["drp"])
-            cd_key = {}
-            piece = T["cdp"] if half != last_half or pairs[-1][0] != "zc" else 1
-            for lo in range(0, POSITIONS, piece):
-                hi = lo + piece
-                key = max(dr_key[hi - 1], ends[("zc", half, hi - 1)] + T["ps"]) + T["ck"]
-                for s in range(lo, hi):
-                    cd_key[s] = key
-                at(key, in_place, "c", half, ALU.subtract, "d", lo, hi)
-            piece = 1 if half == last_half else T["fp"]
-            for lo in range(0, POSITIONS, piece):
-                hi = lo + piece
-                key = max(cd_key[hi - 1], ends[("g2", half, hi - 1)] + T["zl"] + T["szl"]) + T["fk"]
-                at(key, in_place, "c", half, ALU.mult, "m", lo, hi)
-                at(key + 0.1, in_place, "c", half, ALU.add, "d", lo, hi)
-                at(key + 0.1, store, half, lo, hi)
-
         with tc.manual_schedule(engines={mybir.EngineType.PE}):
-            for key, n, fn, args in sorted(events, key=lambda e: (e[0], e[1])):
-                fn(*args)
+            widen_up_to(2 * TILES)
+            for i in range(x_first["tiles"]):
+                turn(x_first, i)
+                if i == 1:
+                    nc.scalar.copy(out=scales[:, 1, :], in_=scales[:, 0, :])
+            turn(x_last, 0)
+            widen_up_to(3 * TILES + 2)
+            quantise(x_first)
+            quantise(x_last)
+            widen_up_to(6 * TILES)
+            turn_next(1)
+            while turned[0] < TURNED_AHEAD:
+                ready = list(complete)
+                turn_next(2)
+                quantise_complete(ready)
+            for pr in pairs:
+                for s in range(POSITIONS):
+                    ready = list(complete)
+                    turn_next(1)
+                    while before_plane and before_plane[0][0] == now[0]:
+                        difference(before_plane.pop(0)[1], 0)
+                    turn_next(1)
+                    if pr is pairs[-1] and s == POSITIONS - 1:
+                        run_later()
+                        last_plane(pr, s, 0, HALF // 2)
+                        now[0] += 1
+                        run_later()
+                        last_plane(pr, s, HALF // 2, HALF // 2)
+                    else:
+                        multiply(pr, s)
+                        quantise_complete(ready)
+                        run_later()
+                        now[0] += 1
+            while later:
+                run_later()
+                now[0] += 1

from contextlib import ExitStack

import concourse.mybir as mybir
from concourse.masks import make_identity

FLOPS = 2 * 512 * 4096 * 2048

F32 = mybir.dt.float32
BF16 = mybir.dt.bfloat16
U32 = mybir.dt.uint32
U8 = mybir.dt.uint8
FP8 = mybir.dt.float8_e4m3fn
FP8X4 = mybir.dt.float8_e4m3fn_x4
ALU = mybir.AluOpType
ACT = mybir.ActivationFunctionType

P = 128
K = 1024
HALF = 512
TILES = 4
POSITIONS = 4

PAIR_ORDER = (("g1", 0), ("g0", 0), ("g1", 1), ("g0", 1), ("zc", 0), ("g2", 0), ("zc", 1), ("g2", 1))

TURNED_AHEAD = 21
WIDENED_AHEAD = 7


def tile_grconv_pa_kernel(tc, x, x_mix, WL, WR, GL, GR_bytes, GR_scale, out):
    nc = tc.nc
    with ExitStack() as ctx:
        const = ctx.enter_context(tc.tile_pool(name="const", bufs=1))
        rows_pool = ctx.enter_context(tc.tile_pool(name="rows_pool", bufs=4))
        bytes_pool = ctx.enter_context(tc.tile_pool(name="bytes_pool", bufs=4))
        wide_pool = ctx.enter_context(tc.tile_pool(name="wide_pool", bufs=2))
        grouped_pool = ctx.enter_context(tc.tile_pool(name="grouped_pool", bufs=4))
        codes_pool = ctx.enter_context(tc.tile_pool(name="codes_pool", bufs=6))
        mix_pool = ctx.enter_context(tc.tile_pool(name="mix_pool", bufs=2))
        short_pool = ctx.enter_context(tc.tile_pool(name="short_pool", bufs=1))
        turn_psum = ctx.enter_context(tc.psum_pool(name="turn_psum", bufs=5))
        plane_psum = ctx.enter_context(tc.psum_pool(name="plane_psum", bufs=3))

        x_view = x.rearrange("s a b k -> (a b) s k")
        mix_view = x_mix.rearrange("s a b h -> (a b) s h")
        out_view = out.rearrange("s a b h -> (a b) s h")

        ident_f32 = const.tile([P, P], F32, name="ident_f32")
        make_identity(nc, ident_f32[:])
        ident_bf16 = const.tile([P, P], BF16, name="ident_bf16")
        make_identity(nc, ident_bf16[:])
        minus_ident = const.tile([P, P], BF16, name="minus_ident")
        nc.vector.tensor_scalar(out=minus_ident[:], in0=ident_bf16[:], scalar1=-1.0, scalar2=None, op0=ALU.mult)
        zero_col = const.tile([P, 1], F32, name="zero_col")
        nc.gpsimd.memset(zero_col[:], 0.0)
        table_warm = const.tile([P, 1], F32, name="table_warm")
        nc.scalar.activation(out=table_warm[:], in_=zero_col[:], func=ACT.Sigmoid)

        seeds = const.tile([P, 8], F32, name="seeds")
        nc.sync.dma_start(
            out=seeds[:].rearrange("p (h j) -> p h j", j=4),
            in_=GR_scale.rearrange("o (h p j) -> (o p) h j", h=2, j=4),
        )
        scales = const.tile([P, 2, K], F32, name="scales")
        seed_banks = []
        for h in range(2):
            seed_bank = turn_psum.tile([P, 512], F32, name="bank", tag="bank")
            for j in range(4):
                nc.tensor.transpose(
                    seed_bank[:, j * P : (j + 1) * P],
                    seeds[:, 4 * h + j : 4 * h + j + 1].to_broadcast([P, P]),
                    ident_f32[:],
                )
            seed_banks.append(seed_bank[:].rearrange("p (j n) -> p n j", j=4))
        nc.vector.tensor_copy(out=scales[:, 0, 0:512], in_=seed_banks[0])
        nc.scalar.copy(out=scales[:, 0, 512:K], in_=seed_banks[1])
        mix_rows = const.tile([P, POSITIONS + 1, K], BF16, name="mix_rows")

        def weight_group(name, dram, first_row, from_bytes):
            return {
                "name": name,
                "src": dram[first_row : first_row + HALF, :].rearrange("(i p) k -> p i k", p=P),
                "from_bytes": from_bytes,
                "tiles": TILES,
            }

        x_first = {"name": "x_first", "src": x_view[:, 0:4, :], "from_bytes": False, "tiles": 4}
        x_last = {"name": "x_last", "src": x_view[:, 4:5, :], "from_bytes": False, "tiles": 1}

        def make_pair(kind, half):
            if kind == "zc":
                first_row = half * HALF
                return (
                    kind,
                    half,
                    weight_group("wl_%d" % half, WL, first_row, False),
                    weight_group("wr_%d" % half, WR, first_row, False),
                )
            first_row = int(kind[1]) * 1024 + half * HALF
            return (
                kind,
                half,
                weight_group("gl_%s_%d" % (kind, half), GL, first_row, False),
                weight_group("gr_%s_%d" % (kind, half), GR_bytes, first_row, True),
            )

        pairs = [make_pair(kind, half) for kind, half in PAIR_ORDER]
        last_half = PAIR_ORDER[-1][1]
        weight_groups = []
        for pr in pairs:
            weight_groups.extend([pr[2], pr[3]])
        rows_to_load = [x_first, x_last] + [g for g in weight_groups if not g["from_bytes"]]
        bytes_to_load = [g for g in weight_groups if g["from_bytes"]]
        piecewise = (x_first["name"], pairs[0][2]["name"], pairs[0][3]["name"])
        mix_follows = pairs[4][2]["name"]

        def load(dst, g):
            if g["name"] in piecewise:
                for i in range(g["tiles"]):
                    nc.sync.dma_start(out=dst[:, i, :], in_=g["src"][:, i, :])
            else:
                nc.sync.dma_start(out=dst[:], in_=g["src"])

        def load_next_rows():
            if not rows_to_load:
                return
            g = rows_to_load.pop(0)
            rows = rows_pool.tile([P, g["tiles"], K], BF16, name="rows", tag="rows")
            load(rows, g)
            g["rows"] = rows
            if g["name"] == mix_follows:
                nc.sync.dma_start(out=mix_rows[:], in_=mix_view)

        def load_next_bytes():
            if not bytes_to_load:
                return
            g = bytes_to_load.pop(0)
            gr_bytes = bytes_pool.tile([P, TILES, K], U8, name="gr_bytes", tag="gr_bytes")
            load(gr_bytes, g)
            g["gr_bytes"] = gr_bytes

        tiles_to_turn = [(g, i) for g in weight_groups for i in range(TILES)]
        tiles_to_widen = [n for n, (g, i) in enumerate(tiles_to_turn) if g["from_bytes"]]

        def product(g, i, n, lo, hi):
            nc.vector.tensor_tensor(
                out=g["rows"][:, i : i + n, lo:hi],
                in0=g["gr_bytes"][:, i : i + n, lo:hi].bitcast(FP8),
                in1=scales[:, 0:n, lo:hi],
                op=ALU.mult,
            )

        def widen_up_to(number):
            while tiles_to_widen and tiles_to_widen[0] < number:
                g, i = tiles_to_turn[tiles_to_widen[0]]
                if i == 0:
                    wide = wide_pool.tile([P, TILES, K], BF16, name="wide", tag="wide")
                    g["rows"] = wide
                if g["name"] not in piecewise:
                    step = 2
                    product(g, i, step, 0, K)
                elif i == 0:
                    step = 1
                    product(g, i, step, 0, 512)
                    product(g, i, step, 512, K)
                else:
                    step = 1
                    product(g, i, step, 0, K)
                for n in range(step):
                    tiles_to_widen.pop(0)
                if i + step == TILES:
                    load_next_bytes()

        def turn(g, i):
            n = g["tiles"]
            if i == 0:
                grouped = grouped_pool.tile([P, n * K], BF16, name="grouped", tag="grouped", align_bytes=64)
                g["grouped"] = grouped
            grouped_words = g["grouped"][:].bitcast(F32).rearrange("p (g i r u) -> p g i r u", g=2, i=n, u=2)
            words = g["rows"][:, i, :].bitcast(F32)
            bank = turn_psum.tile([P, 512], F32, name="bank", tag="bank")
            for g2 in range(2):
                for u in range(2):
                    c = 2 * g2 + u
                    nc.tensor.transpose(
                        bank[:, c * P : (c + 1) * P],
                        words[:, 256 * g2 + u : 256 * (g2 + 1) : 2],
                        ident_f32[:],
                    )
            nc.scalar.copy(
                out=grouped_words[:, :, i, :, :],
                in_=bank[:].rearrange("p (g u r) -> p g r u", g=2, u=2),
            )
            if i == n - 1 and not g["from_bytes"]:
                load_next_rows()

        def quantise(g):
            n = g["tiles"]
            if n == TILES and g["name"] != x_first["name"]:
                codes = codes_pool.tile([P, n * 256], U32, name="codes", tag="codes", align_bytes=64)
                blocks = codes_pool.tile([P, n * 256], U8, name="blocks", tag="blocks", align_bytes=64)
            else:
                codes = const.tile([P, n * 256], U32, name="codes_" + g["name"], align_bytes=64)
                blocks = const.tile([P, n * 256], U8, name="blocks_" + g["name"], align_bytes=64)
            nc.vector.quantize_mx(out=codes[:].bitcast(FP8X4), scales=blocks[:], in_=g["grouped"][:])
            g["codes"] = codes
            g["blocks"] = blocks

        turned = [0]
        complete = []

        def turn_next(count):
            for number in range(turned[0], min(turned[0] + count, len(tiles_to_turn))):
                g, i = tiles_to_turn[number]
                turn(g, i)
                widen_up_to(number + WIDENED_AHEAD)
                if i == TILES - 1:
                    complete.append(g)
            turned[0] += count

        def quantise_complete(groups):
            for g in groups:
                quantise(g)
                complete.pop(0)

        def x_operand(pos, g2):
            if pos < 4:
                lo = g2 * 512 + pos * P
                return x_first["codes"][:, lo : lo + P], x_first["blocks"][:, lo : lo + P]
            lo = g2 * P
            return x_last["codes"][:, lo : lo + P], x_last["blocks"][:, lo : lo + P]

        def plane(s, left_group, right_group, lo=0, width=HALF):
            acc = plane_psum.tile([P, width], F32, name="acc", tag="acc")
            passes = [(s, 0, left_group), (s, 1, left_group), (s + 1, 0, right_group), (s + 1, 1, right_group)]
            for n, (pos, g2, grp) in enumerate(passes):
                x_codes, x_blocks = x_operand(pos, g2)
                nc.tensor.matmul_mx(
                    out=acc[:],
                    lhsT=x_codes.bitcast(FP8X4),
                    lhsT_scale=x_blocks,
                    rhs=grp["codes"][:, g2 * HALF + lo : g2 * HALF + lo + width].bitcast(FP8X4),
                    rhs_scale=grp["blocks"][:, g2 * HALF + lo : g2 * HALF + lo + width],
                    start=(n == 0),
                    stop=(n == 3),
                )
            return acc

        mix = {}

        def mix_tile(name, half):
            pool = short_pool if name in ("g1", "u") else mix_pool
            t = pool.tile([P, POSITIONS, HALF], F32, name=name, tag=name)
            mix[(name, half)] = t

        def columns(half):
            return slice(half * HALF, (half + 1) * HALF)

        later = []
        before_plane = []
        now = [0]
        done = {}

        def after(planes, step, *args):
            later.append((now[0] + planes, step, args))

        def run_later():
            due = [e for e in later if e[0] <= now[0]]
            while due:
                rest = [e for e in later if e[0] > now[0]]
                later.clear()
                later.extend(rest)
                for when, step, args in due:
                    step(*args)
                due = [e for e in later if e[0] <= now[0]]

        def tensor(out_ap, in0, in1, op):
            nc.vector.tensor_tensor(out=out_ap, in0=in0, in1=in1, op=op)

        def share(half, s):
            d = mix[("d", half)][:, s, :]
            nc.scalar.activation(out=d, in_=d, func=ACT.Sigmoid)
            if s % 2 == 1:
                after(1, distance, half, s - 1)

        def distance(half, first):
            d = mix[("d", half)][:, first : first + 2, :]
            nc.scalar.activation(out=mix[("u", half)][:, first : first + 2, :], in_=d, func=ACT.Abs, bias=-0.5)
            if first + 2 == POSITIONS:
                before_plane.append((now[0] + 1, half))
                for s in range(1, POSITIONS):
                    after(1, difference, half, s)
                done[("distance", half)] = True
                if ("distance", 1 - half) in done:
                    for h in range(2):
                        after(1, logarithm, h)

        def logarithm(half):
            u = mix[("u", half)]
            nc.scalar.activation(out=u[:], in_=u[:], func=ACT.Ln, bias=0.5)
            after(1, log_sum, half)

        def difference(half, s):
            diff = plane_psum.tile([P, HALF], F32, name="acc", tag="acc")
            cols = columns(half)
            nc.tensor.matmul(diff[:], lhsT=ident_bf16[:], rhs=mix_rows[:, s, cols], start=True, stop=False)
            nc.tensor.matmul(diff[:], lhsT=minus_ident[:], rhs=mix_rows[:, s + 1, cols], start=False, stop=True)
            after(0, scale_difference, half, s, diff)

        def scale_difference(half, s, diff):
            d = mix[("d", half)][:, s, :]
            tensor(d, d, diff[:], ALU.mult)
            if s == POSITIONS - 1:
                after(1, left_right, half)

        def left_right(half):
            d = mix[("d", half)]
            tensor(d[:], d[:], mix_rows[:, 1 : POSITIONS + 1, columns(half)], ALU.add)

        def log_sum(half):
            m = mix[("m", half)]
            tensor(m[:], m[:], mix[("u", half)][:], ALU.subtract)

        def center_less_y(half, first):
            c, d = [mix[(name, half)][:, first : first + 2, :] for name in ("c", "d")]
            tensor(c, c, d, ALU.subtract)

        def finish(half, first, last, lo=0, width=HALF):
            c, m, d = [mix[(name, half)][:, first:last, lo : lo + width] for name in ("c", "m", "d")]
            tensor(c, c, m, ALU.mult)
            tensor(c, c, d, ALU.add)
            column = half * HALF + lo
            nc.sync.dma_start(out=out_view[:, first:last, column : column + width], in_=c)

        def weight(half, first, last):
            m = mix[("m", half)][:, first:last, :]
            nc.scalar.activation(out=m, in_=m, func=ACT.Sigmoid)
            after(1, finish, half, first, last)

        def last_plane(pr, s, lo, width):
            kind, half, left_group, right_group = pr
            acc = plane(s, left_group, right_group, lo, width)
            m = mix[("m", half)][:, s, lo : lo + width]
            tensor(m, acc[:], m, ALU.subtract)
            nc.scalar.activation(out=m, in_=m, func=ACT.Sigmoid)
            finish(half, s, s + 1, lo, width)

        def multiply(pr, s):
            kind, half, left_group, right_group = pr
            if s == 0:
                for name in {"zc": ("c",), "g1": ("g1",), "g0": ("d", "m", "u"), "g2": ()}[kind]:
                    mix_tile(name, half)
            acc = plane(s, left_group, right_group)
            after(1, first_step, kind, half, s, acc)

        def first_step(kind, half, s, acc):
            if kind == "zc":
                nc.scalar.activation(out=mix[("c", half)][:, s, :], in_=acc[:], func=ACT.Sigmoid)
                if s % 2 == 1:
                    after(3, center_less_y, half, s - 1)
            elif kind == "g1":
                nc.scalar.copy(out=mix[("g1", half)][:, s, :], in_=acc[:])
            elif kind == "g0":
                g1, d, m = [mix[(name, half)][:, s, :] for name in ("g1", "d", "m")]
                tensor(d, acc[:], g1, ALU.subtract)
                tensor(m, acc[:], g1, ALU.max)
                after(0, share, half, s)
            else:
                m = mix[("m", half)][:, s, :]
                tensor(m, acc[:], m, ALU.subtract)
                if half == last_half:
                    after(0, weight, half, s, s + 1)
                elif s % 2 == 1:
                    after(0, weight, half, s - 1, s + 1)

        load_next_bytes()
        load_next_bytes()
        for n in range(4):
            load_next_rows()
        for n in range(2):
            load_next_bytes()

        with tc.manual_schedule(engines={mybir.EngineType.PE}):
            widen_up_to(2 * TILES)
            for i in range(x_first["tiles"]):
                turn(x_first, i)
                if i == 1:
                    nc.scalar.copy(out=scales[:, 1, :], in_=scales[:, 0, :])
            turn(x_last, 0)
            widen_up_to(3 * TILES + 2)
            quantise(x_first)
            quantise(x_last)
            widen_up_to(6 * TILES)
            turn_next(1)
            while turned[0] < TURNED_AHEAD:
                ready = list(complete)
                turn_next(2)
                quantise_complete(ready)
            for pr in pairs:
                for s in range(POSITIONS):
                    ready = list(complete)
                    turn_next(1)
                    while before_plane and before_plane[0][0] == now[0]:
                        difference(before_plane.pop(0)[1], 0)
                    turn_next(1)
                    if pr is pairs[-1] and s == POSITIONS - 1:
                        run_later()
                        last_plane(pr, s, 0, HALF // 2)
                        now[0] += 1
                        run_later()
                        last_plane(pr, s, HALF // 2, HALF // 2)
                    else:
                        multiply(pr, s)
                        quantise_complete(ready)
                        run_later()
                        now[0] += 1
            while later:
                run_later()
                now[0] += 1
